import numpy as np
import ml_dtypes


def mxq(x, axis, fmt="e4m3"):
    dtype, down = {"e4m3": (ml_dtypes.float8_e4m3fn, 7), "e5m2": (ml_dtypes.float8_e5m2, 14)}[fmt]
    v = np.moveaxis(np.asarray(x, np.float32).astype(ml_dtypes.bfloat16).astype(np.float64), axis, -1)
    blocks = v.reshape(v.shape[:-1] + (-1, 32))
    amax = np.abs(blocks).max(-1, keepdims=True)
    byte = np.maximum(np.where(amax > 0, np.frexp(amax)[1] - 1 + 127, 0) - down, 1)
    scale = np.exp2(byte - 127.0)
    codes = (blocks / scale).astype(np.float32).astype(dtype).astype(np.float64)
    return np.moveaxis((codes * scale).reshape(v.shape), -1, axis)


WIDE = False


def mx_kscale(k):
    if not WIDE:
        return np.ones(k)
    levels = np.array([10, -10, 5, -5, 0])
    a = np.random.permutation(np.resize(levels, k // 512 * 4)).reshape(k // 512, 4)
    idx = np.arange(k)
    return np.exp2(a[idx // 512, idx % 128 // 32])


BF16 = ml_dtypes.bfloat16


def bf(x):
    return np.asarray(x, np.float32).astype(BF16)


def f64(x):
    return np.asarray(x).astype(np.float64)


B, T, D, H, DK, ROPE, NOPE, VD, KVR, QR = 1, 8192, 512, 2, 128, 64, 64, 128, 512, 1024
EPS = 1.1920928955078125e-07
HALF = ROPE // 2


def rms_norm(h, w):
    var = np.mean(h * h, axis=-1, keepdims=True)
    return h * (1.0 / np.sqrt(var + EPS)) * w


def rope(v):
    inv_freq = 1.0 / (10000.0 ** (f64(np.arange(0, ROPE, 2)) / ROPE))
    freqs = np.outer(f64(np.arange(v.shape[-2])), inv_freq)
    cos, sin = np.cos(freqs), np.sin(freqs)
    v1, v2 = v[..., :HALF], v[..., HALF:]
    return np.concatenate([v1 * cos - v2 * sin, v1 * sin + v2 * cos], axis=-1)


def setup_inputs():
    s, t = mx_kscale(D), mx_kscale(KVR)
    return {'x': bf(np.random.standard_normal((B, T, D)) * s),
            'wkv_c': bf(np.random.standard_normal((D, KVR)) / np.sqrt(D) / s[:, None]),
            'kv_a_norm_w': bf((1.0 + 0.1 * np.random.standard_normal(KVR)) * t),
            'wkv_b': bf(np.random.standard_normal((KVR, H * (NOPE + VD))) / np.sqrt(KVR) / t[:, None]),
            'k_pe': bf(np.random.standard_normal((B, T, ROPE)))}


def reference(x, wkv_c, kv_a_norm_w, wkv_b, k_pe):
    c = mxq(f64(x), 2, 'e4m3') @ mxq(f64(wkv_c), 0, 'e4m3')
    cn = rms_norm(c, f64(kv_a_norm_w))
    kv = mxq(cn, 2, 'e4m3') @ mxq(f64(wkv_b), 0, 'e4m3')
    kv = kv.reshape(B, T, H, NOPE + VD).transpose(0, 2, 1, 3)
    k_nope, v = kv[..., :NOPE], kv[..., NOPE:]
    k_rot = rope(f64(k_pe)[:, None])
    k_rot = np.broadcast_to(k_rot, (B, H, T, ROPE))
    ks = np.concatenate([k_nope, k_rot], axis=-1)
    return ks, np.ascontiguousarray(v)

@@ -1,0 +1,296 @@
+from contextlib import ExitStack
+
+import concourse.bass as bass
+import concourse.mybir as mybir
+import concourse.tile as tile
+from concourse.masks import make_identity
+
+F32 = mybir.dt.float32
+BF16 = mybir.dt.bfloat16
+U32 = mybir.dt.uint32
+U8 = mybir.dt.uint8
+I32 = mybir.dt.int32
+FP8X4 = mybir.dt.float8_e4m3fn_x4
+ALU = mybir.AluOpType
+ACT = mybir.ActivationFunctionType
+
+P = 128
+T = 8192
+D = 512
+KVR = 512
+H = 2
+NOPE = 64
+VD = 128
+ROPE = 64
+HALF = 32
+EPS = 1.1920928955078125e-07
+PI = 3.141592653589793
+TPP = T // P
+CH = 8
+NCH = TPP // CH
+NPAIR = TPP // 2
+PPC = CH // 2
+
+FLOPS = 2 * T * D * KVR + 2 * T * KVR * H * (NOPE + VD)
+MANUAL = False
+
+
+def tile_deepseekmultiheadattention_pb_t_kernel(tc, x, wkv_c, kv_a_norm_w, wkv_b, k_pe, out_0, out_1):
+    nc = tc.nc
+    xv = x.flatten_outer_dims().rearrange("(p i) k -> p i k", i=TPP)
+    kpv = k_pe.flatten_outer_dims().rearrange("(p i) k -> p i k", i=TPP)
+    ksv = out_0.rearrange("o h (p i) d -> p (o h) i d", i=TPP)
+    vv = out_1.rearrange("o h (p i) d -> p (o h) i d", i=TPP)
+
+    with ExitStack() as ctx:
+        const = ctx.enter_context(tc.tile_pool(name="const", bufs=1))
+        xin = ctx.enter_context(tc.tile_pool(name="xin", bufs=4))
+        work = ctx.enter_context(tc.tile_pool(name="work", bufs=3))
+        small = ctx.enter_context(tc.tile_pool(name="small", bufs=4))
+        vout = ctx.enter_context(tc.tile_pool(name="vout", bufs=3))
+        ropet = ctx.enter_context(tc.tile_pool(name="ropet", bufs=2))
+        psum = ctx.enter_context(tc.psum_pool(name="psum", bufs=1))
+        if MANUAL:
+            ctx.enter_context(tc.manual_schedule())
+
+        x_tiles = {}
+
+        def load_x(c, pieces):
+            xc = xin.tile([P, CH, D], BF16, name="xc")
+            lo = 0
+            for n in pieces:
+                nc.sync.dma_start(out=xc[:, lo:lo + n, :], in_=xv[:, c * CH + lo:c * CH + lo + n, :])
+                lo += n
+            x_tiles[c] = xc
+
+        wc_raw = const.tile([P, 4, KVR], BF16, name="wc_raw")
+        wb_raw = const.tile([P, 4, H * (NOPE + VD)], BF16, name="wb_raw")
+        gain_b = const.tile([P, KVR], BF16, name="gain_b")
+        kpe_sb = const.tile([P, TPP, ROPE], BF16, name="kpe_sb")
+
+        load_x(0, [2, 6])
+        for u in range(2):
+            nc.scalar.dma_start(out=wc_raw[:, 2 * u:2 * u + 2, :],
+                                in_=wkv_c[256 * u:256 * u + 256, :].rearrange("(p e) f -> p e f", e=2))
+        nc.scalar.dma_start(out=gain_b[:], in_=kv_a_norm_w.partition_broadcast(P))
+        nc.scalar.dma_start(out=wb_raw[:], in_=wkv_b.rearrange("(t p) c -> p t c", p=P))
+        load_x(1, [CH])
+        nc.sync.dma_start(out=kpe_sb[:], in_=kpv)
+        load_x(2, [CH])
+        load_x(3, [CH])
+
+        ident_f = const.tile([P, P], F32, name="ident_f")
+        make_identity(nc, ident_f[:])
+        ident_b = const.tile([P, P], BF16, name="ident_b")
+        make_identity(nc, ident_b[:])
+        eps_t = const.tile([P, 1], F32, name="eps_t")
+        nc.vector.memset(eps_t[:], EPS)
+        one_t = const.tile([P, 1], F32, name="one_t")
+        nc.vector.memset(one_t[:], 1.0)
+
+        wcq = const.tile([P, KVR], U32, name="wcq", align_bytes=64)
+        wcs = const.tile([P, KVR], U8, name="wcs", align_bytes=64)
+        wbvq = const.tile([P, H * VD], U32, name="wbvq", align_bytes=64)
+        wbvs = const.tile([P, H * VD], U8, name="wbvs", align_bytes=64)
+        wbkq = const.tile([P, H * NOPE], U32, name="wbkq", align_bytes=64)
+        wbks = const.tile([P, H * NOPE], U8, name="wbks", align_bytes=64)
+
+        def prep_wc():
+            wc_g = const.tile([P, KVR, 4], BF16, name="wc_g", align_bytes=64)
+            nc.vector.tensor_copy(out=wc_g[:], in_=wc_raw[:].rearrange("p t f -> p f t"))
+            nc.vector.quantize_mx(out=wcq[:].bitcast(FP8X4), scales=wcs[:],
+                                  in_=wc_g[:].rearrange("p f t -> p (f t)"))
+
+        def prep_wb():
+            wbh = wb_raw[:].rearrange("p t (h c) -> p t h c", h=H)
+            wbv_g = const.tile([P, H, VD, 4], BF16, name="wbv_g", align_bytes=64)
+            wbk_g = const.tile([P, H, NOPE, 4], BF16, name="wbk_g", align_bytes=64)
+            nc.vector.tensor_copy(out=wbv_g[:], in_=wbh[:, :, :, NOPE:NOPE + VD].rearrange("p t h c -> p h c t"))
+            nc.vector.tensor_copy(out=wbk_g[:], in_=wbh[:, :, :, 0:NOPE].rearrange("p t h c -> p h c t"))
+            nc.vector.quantize_mx(out=wbvq[:].bitcast(FP8X4), scales=wbvs[:],
+                                  in_=wbv_g[:].rearrange("p h c t -> p (h c t)"))
+            nc.vector.quantize_mx(out=wbkq[:].bitcast(FP8X4), scales=wbks[:],
+                                  in_=wbk_g[:].rearrange("p h c t -> p (h c t)"))
+
+        t_f = const.tile([P, TPP], F32, name="t_f")
+        g_b = const.tile([P, HALF], F32, name="g_b")
+        turns = const.tile([P, TPP, HALF], F32, name="turns")
+        whole = const.tile([P, TPP, HALF], I32, name="whole")
+        sin_t = const.tile([P, TPP, HALF], F32, name="sin_t")
+        cos_t = const.tile([P, TPP, HALF], F32, name="cos_t")
+
+        def table_start():
+            nc.gpsimd.iota(t_f[:], pattern=[[1, TPP]], base=0, channel_multiplier=TPP,
+                           allow_small_or_imprecise_dtypes=True)
+            for j in range(HALF):
+                g = 10000.0 ** (-j / float(HALF)) / (2.0 * PI)
+                nc.vector.tensor_scalar(out=g_b[:, j:j + 1], in0=one_t[:], scalar1=g, scalar2=None, op0=ALU.mult)
+            nc.gpsimd.tensor_tensor(out=turns[:], in0=t_f[:].unsqueeze(2).to_broadcast([P, TPP, HALF]),
+                                    in1=g_b[:].unsqueeze(1).to_broadcast([P, TPP, HALF]), op=ALU.mult)
+            nc.gpsimd.tensor_scalar(out=whole[:], in0=turns[:], scalar1=1.0, scalar2=0.0, op0=ALU.mult, op1=ALU.add)
+
+        def table_mid():
+            nc.vector.tensor_tensor(out=turns[:], in0=turns[:], in1=whole[:], op=ALU.subtract)
+
+        def table_end():
+            nc.scalar.activation(out=sin_t[:], in_=turns[:], func=ACT.Sin, scale=2.0 * PI)
+            nc.scalar.activation(out=cos_t[:], in_=turns[:], func=ACT.Sin, scale=PI)
+            nc.gpsimd.tensor_tensor(out=cos_t[:], in0=cos_t[:], in1=cos_t[:], op=ALU.mult)
+            nc.gpsimd.tensor_scalar(out=cos_t[:], in0=cos_t[:], scalar1=-2.0, scalar2=1.0, op0=ALU.mult, op1=ALU.add)
+
+        ks_tiles = {}
+        for c in range(NCH):
+            ks_tiles[c] = const.tile([P, H, CH, NOPE + ROPE], F32, name="ks%d" % c)
+
+        def rope(c):
+            kp = kpe_sb[:, c * CH:(c + 1) * CH, :].rearrange("p i (s j) -> p i s j", s=2)
+            cs = cos_t[:, c * CH:(c + 1) * CH, :]
+            sn = sin_t[:, c * CH:(c + 1) * CH, :]
+            pc = ropet.tile([P, CH, 2, HALF], F32, name="pc")
+            ps = ropet.tile([P, CH, 2, HALF], F32, name="ps")
+            nc.gpsimd.tensor_tensor(out=pc[:], in0=kp, in1=cs.unsqueeze(2).to_broadcast([P, CH, 2, HALF]), op=ALU.mult)
+            nc.gpsimd.tensor_tensor(out=ps[:], in0=kp, in1=sn.unsqueeze(2).to_broadcast([P, CH, 2, HALF]), op=ALU.mult)
+            kst = ks_tiles[c]
+            shp = [P, H, CH, HALF]
+            nc.gpsimd.tensor_tensor(out=kst[:, :, :, NOPE:NOPE + HALF],
+                                    in0=pc[:, :, 0, :].unsqueeze(1).to_broadcast(shp),
+                                    in1=ps[:, :, 1, :].unsqueeze(1).to_broadcast(shp), op=ALU.subtract)
+            nc.gpsimd.tensor_tensor(out=kst[:, :, :, NOPE + HALF:NOPE + ROPE],
+                                    in0=ps[:, :, 0, :].unsqueeze(1).to_broadcast(shp),
+                                    in1=pc[:, :, 1, :].unsqueeze(1).to_broadcast(shp), op=ALU.add)
+
+        st = {}
+
+        def stage_a(n):
+            xc = x_tiles[n // PPC]
+            xt = psum.tile([P, 2, 2, P], F32, name="xt")
+            for a in range(2):
+                xw = xc[:, 2 * (n % PPC) + a, :].bitcast(F32)
+                for u in range(2):
+                    nc.tensor.transpose(xt[:, a, u, :], xw[:, P * u:P * u + P], ident_f[:])
+            st["xt", n] = xt
+
+        def stage_b_exit(n):
+            gx = work.tile([P, 2 * P * 4], BF16, name="gx", align_bytes=64)
+            nc.scalar.copy(out=gx[:].bitcast(F32).rearrange("p (a r u) -> p a r u", a=2, u=2),
+                           in_=st["xt", n][:].rearrange("p a u r -> p a r u"))
+            st["gx", n] = gx
+
+        def stage_b_quant(n):
+            xq = work.tile([P, 2 * P], U32, name="xq", align_bytes=64)
+            xs = work.tile([P, 2 * P], U8, name="xs", align_bytes=64)
+            nc.vector.quantize_mx(out=xq[:].bitcast(FP8X4), scales=xs[:], in_=st["gx", n][:])
+            st["xq", n] = (xq, xs)
+
+        def stage_c(n):
+            xq, xs = st["xq", n]
+            for a in range(2):
+                cb = psum.tile([P, KVR], F32, name="cb", bufs=4)
+                nc.tensor.matmul_mx(out=cb[:], lhsT=xq[:, P * a:P * a + P].bitcast(FP8X4), lhsT_scale=xs[:, P * a:P * a + P],
+                                    rhs=wcq[:].bitcast(FP8X4), rhs_scale=wcs[:], start=True, stop=True)
+                st["cb", n, a] = cb
+
+        def stage_d(n):
+            ss = small.tile([P, 2], F32, name="ss")
+            for a in range(2):
+                sq = work.tile([P, KVR], BF16, name="sq")
+                nc.scalar.activation(out=sq[:], in_=st["cb", n, a][:], func=ACT.Square, accum_out=ss[:, a:a + 1])
+            rms = small.tile([P, 2], F32, name="rms")
+            nc.scalar.activation(out=rms[:], in_=ss[:], func=ACT.Sqrt, scale=1.0 / KVR, bias=eps_t[:])
+            st["rms", n] = rms
+
+        def stage_e(n):
+            rstd = small.tile([P, 2], F32, name="rstd")
+            nc.vector.reciprocal(out=rstd[:], in_=st["rms", n][:])
+            cn = work.tile([P, 2, KVR], BF16, name="cn")
+            for a in range(2):
+                nc.vector.scalar_tensor_tensor(out=cn[:, a, :], in0=st["cb", n, a][:], scalar=rstd[:, a:a + 1],
+                                               in1=gain_b[:], op0=ALU.mult, op1=ALU.mult)
+            st["cn", n] = cn
+
+        def stage_f(n):
+            cn = st["cn", n]
+            ct = psum.tile([P, 2, 4, P], BF16, name="ct")
+            for a in range(2):
+                for t in range(4):
+                    nc.tensor.transpose(ct[:, a, t, :], cn[:, a, P * t:P * t + P], ident_b[:])
+            st["ct", n] = ct
+
+        def stage_g_exit(n):
+            gc = work.tile([P, 2, P, 4], BF16, name="gc", align_bytes=64)
+            nc.vector.tensor_copy(out=gc[:], in_=st["ct", n][:].rearrange("p a t r -> p a r t"))
+            st["gc", n] = gc
+
+        def stage_g_quant(n):
+            cq = work.tile([P, 2 * P], U32, name="cq", align_bytes=64)
+            cs = work.tile([P, 2 * P], U8, name="cs", align_bytes=64)
+            nc.vector.quantize_mx(out=cq[:].bitcast(FP8X4), scales=cs[:],
+                                  in_=st["gc", n][:].rearrange("p a r t -> p (a r t)"))
+            st["cq", n] = (cq, cs)
+
+        def stage_h(n):
+            cq, cs = st["cq", n]
+            pv = psum.tile([P, 2, H * VD], F32, name="pv")
+            pk = psum.tile([P, 2, H * NOPE], F32, name="pk")
+            for a in range(2):
+                nc.tensor.matmul_mx(out=pv[:, a, :], lhsT=cq[:, P * a:P * a + P].bitcast(FP8X4), lhsT_scale=cs[:, P * a:P * a + P],
+                                    rhs=wbvq[:].bitcast(FP8X4), rhs_scale=wbvs[:], start=True, stop=True)
+                nc.tensor.matmul_mx(out=pk[:, a, :], lhsT=cq[:, P * a:P * a + P].bitcast(FP8X4), lhsT_scale=cs[:, P * a:P * a + P],
+                                    rhs=wbkq[:].bitcast(FP8X4), rhs_scale=wbks[:], start=True, stop=True)
+            st["pv", n] = pv
+            st["pk", n] = pk
+
+        v_tiles = {}
+
+        def stage_i(n):
+            c = n // PPC
+            i0 = 2 * (n % PPC)
+            if n % PPC == 0:
+                v_tiles[c] = vout.tile([P, H, CH, VD], F32, name="vt")
+            vt = v_tiles[c]
+            nc.scalar.copy(out=vt[:, :, i0:i0 + 2, :], in_=st["pv", n][:].rearrange("p a (h d) -> p h a d", h=H))
+            nc.scalar.copy(out=ks_tiles[c][:, :, i0:i0 + 2, 0:NOPE],
+                           in_=st["pk", n][:].rearrange("p a (h d) -> p h a d", h=H))
+            if n % PPC == PPC - 1:
+                nc.sync.dma_start(out=vv[:, :, c * CH:(c + 1) * CH, :], in_=vt[:])
+                nc.sync.dma_start(out=ksv[:, :, c * CH:(c + 1) * CH, :], in_=ks_tiles[c][:])
+
+        table_start()
+        prep_wc()
+
+        def on(n):
+            return 0 <= n < NPAIR
+
+        for k in range(NPAIR + 6):
+            if on(k):
+                stage_a(k)
+                if k % PPC == PPC - 1 and k // PPC + 4 < NCH:
+                    load_x(k // PPC + 4, [CH])
+            if on(k - 3):
+                stage_f(k - 3)
+            if on(k - 5):
+                stage_i(k - 5)
+            if on(k):
+                stage_b_exit(k)
+            if on(k - 2):
+                stage_e(k - 2)
+            if on(k - 3):
+                stage_g_exit(k - 3)
+            if on(k):
+                stage_b_quant(k)
+            if on(k - 3):
+                stage_g_quant(k - 3)
+            if k == 1:
+                prep_wb()
+            if k == 2:
+                table_mid()
+            if on(k - 1):
+                stage_c(k - 1)
+            if on(k - 4):
+                stage_h(k - 4)
+            if on(k - 1):
+                stage_d(k - 1)
+            if k == 3:
+                table_end()
+            if k >= 4 and k - 4 < NCH:
+                rope(k - 4)

@@ -1,8 +1,6 @@
 from contextlib import ExitStack
 
-import concourse.bass as bass
 import concourse.mybir as mybir
-import concourse.tile as tile
 from concourse.masks import make_identity
 
 F32 = mybir.dt.float32
@@ -30,9 +28,13 @@ CH = 8
 NCH = TPP // CH
 NPAIR = TPP // 2
 PPC = CH // 2
+RG = 4
+NRG = TPP // RG
+PW = 2 * P
 
 FLOPS = 2 * T * D * KVR + 2 * T * KVR * H * (NOPE + VD)
-MANUAL = False
+MANUAL = True
+RSQRT = True
 
 
 def tile_deepseekmultiheadattention_pb_t_kernel(tc, x, wkv_c, kv_a_norm_w, wkv_b, k_pe, out_0, out_1):
@@ -118,16 +120,23 @@ def tile_deepseekmultiheadattention_pb_t_kernel(tc, x, wkv_c, kv_a_norm_w, wkv_b
         whole = const.tile([P, TPP, HALF], I32, name="whole")
         sin_t = const.tile([P, TPP, HALF], F32, name="sin_t")
         cos_t = const.tile([P, TPP, HALF], F32, name="cos_t")
+        TG = 8
 
         def table_start():
             nc.gpsimd.iota(t_f[:], pattern=[[1, TPP]], base=0, channel_multiplier=TPP,
                            allow_small_or_imprecise_dtypes=True)
             for j in range(HALF):
                 g = 10000.0 ** (-j / float(HALF)) / (2.0 * PI)
-                nc.vector.tensor_scalar(out=g_b[:, j:j + 1], in0=one_t[:], scalar1=g, scalar2=None, op0=ALU.mult)
-            nc.gpsimd.tensor_tensor(out=turns[:], in0=t_f[:].unsqueeze(2).to_broadcast([P, TPP, HALF]),
-                                    in1=g_b[:].unsqueeze(1).to_broadcast([P, TPP, HALF]), op=ALU.mult)
-            nc.gpsimd.tensor_scalar(out=whole[:], in0=turns[:], scalar1=1.0, scalar2=0.0, op0=ALU.mult, op1=ALU.add)
+                if j < HALF // 2:
+                    nc.vector.tensor_scalar(out=g_b[:, j:j + 1], in0=one_t[:], scalar1=g, scalar2=None, op0=ALU.mult)
+                else:
+                    nc.scalar.mul(out=g_b[:, j:j + 1], in_=one_t[:], mul=g)
+            for lo in range(0, TPP, TG):
+                nc.gpsimd.tensor_tensor(out=turns[:, lo:lo + TG, :],
+                                        in0=t_f[:, lo:lo + TG].unsqueeze(2).to_broadcast([P, TG, HALF]),
+                                        in1=g_b[:].unsqueeze(1).to_broadcast([P, TG, HALF]), op=ALU.mult)
+                nc.gpsimd.tensor_scalar(out=whole[:, lo:lo + TG, :], in0=turns[:, lo:lo + TG, :],
+                                        scalar1=1.0, scalar2=0.0, op0=ALU.mult, op1=ALU.add)
 
         def table_mid():
             nc.vector.tensor_tensor(out=turns[:], in0=turns[:], in1=whole[:], op=ALU.subtract)
@@ -135,23 +144,27 @@ def tile_deepseekmultiheadattention_pb_t_kernel(tc, x, wkv_c, kv_a_norm_w, wkv_b
         def table_end():
             nc.scalar.activation(out=sin_t[:], in_=turns[:], func=ACT.Sin, scale=2.0 * PI)
             nc.scalar.activation(out=cos_t[:], in_=turns[:], func=ACT.Sin, scale=PI)
-            nc.gpsimd.tensor_tensor(out=cos_t[:], in0=cos_t[:], in1=cos_t[:], op=ALU.mult)
-            nc.gpsimd.tensor_scalar(out=cos_t[:], in0=cos_t[:], scalar1=-2.0, scalar2=1.0, op0=ALU.mult, op1=ALU.add)
+            for lo in range(0, TPP, TG):
+                cpart = cos_t[:, lo:lo + TG, :]
+                nc.gpsimd.tensor_tensor(out=cpart, in0=cpart, in1=cpart, op=ALU.mult)
+                nc.gpsimd.tensor_scalar(out=cpart, in0=cpart, scalar1=-2.0, scalar2=1.0, op0=ALU.mult, op1=ALU.add)
 
         ks_tiles = {}
         for c in range(NCH):
             ks_tiles[c] = const.tile([P, H, CH, NOPE + ROPE], F32, name="ks%d" % c)
 
-        def rope(c):
-            kp = kpe_sb[:, c * CH:(c + 1) * CH, :].rearrange("p i (s j) -> p i s j", s=2)
-            cs = cos_t[:, c * CH:(c + 1) * CH, :]
-            sn = sin_t[:, c * CH:(c + 1) * CH, :]
-            pc = ropet.tile([P, CH, 2, HALF], F32, name="pc")
-            ps = ropet.tile([P, CH, 2, HALF], F32, name="ps")
-            nc.gpsimd.tensor_tensor(out=pc[:], in0=kp, in1=cs.unsqueeze(2).to_broadcast([P, CH, 2, HALF]), op=ALU.mult)
-            nc.gpsimd.tensor_tensor(out=ps[:], in0=kp, in1=sn.unsqueeze(2).to_broadcast([P, CH, 2, HALF]), op=ALU.mult)
-            kst = ks_tiles[c]
-            shp = [P, H, CH, HALF]
+        def rope(g):
+            lo = g * RG
+            kp = kpe_sb[:, lo:lo + RG, :].rearrange("p i (s j) -> p i s j", s=2)
+            cs = cos_t[:, lo:lo + RG, :]
+            sn = sin_t[:, lo:lo + RG, :]
+            pc = ropet.tile([P, RG, 2, HALF], F32, name="pc")
+            ps = ropet.tile([P, RG, 2, HALF], F32, name="ps")
+            nc.gpsimd.tensor_tensor(out=pc[:], in0=kp, in1=cs.unsqueeze(2).to_broadcast([P, RG, 2, HALF]), op=ALU.mult)
+            nc.gpsimd.tensor_tensor(out=ps[:], in0=kp, in1=sn.unsqueeze(2).to_broadcast([P, RG, 2, HALF]), op=ALU.mult)
+            i0 = lo % CH
+            kst = ks_tiles[lo // CH][:, :, i0:i0 + RG, :]
+            shp = [P, H, RG, HALF]
             nc.gpsimd.tensor_tensor(out=kst[:, :, :, NOPE:NOPE + HALF],
                                     in0=pc[:, :, 0, :].unsqueeze(1).to_broadcast(shp),
                                     in1=ps[:, :, 1, :].unsqueeze(1).to_broadcast(shp), op=ALU.subtract)
@@ -161,7 +174,15 @@ def tile_deepseekmultiheadattention_pb_t_kernel(tc, x, wkv_c, kv_a_norm_w, wkv_b
 
         st = {}
 
-        def stage_a(n):
+        def on(n):
+            return 0 <= n < NPAIR
+
+        def grouped(k):
+            if ("grp", k) not in st:
+                st["grp", k] = work.tile([P, 2 * PW * 4], BF16, name="grp", align_bytes=64)
+            return st["grp", k]
+
+        def transpose_x(n):
             xc = x_tiles[n // PPC]
             xt = psum.tile([P, 2, 2, P], F32, name="xt")
             for a in range(2):
@@ -170,45 +191,47 @@ def tile_deepseekmultiheadattention_pb_t_kernel(tc, x, wkv_c, kv_a_norm_w, wkv_b
                     nc.tensor.transpose(xt[:, a, u, :], xw[:, P * u:P * u + P], ident_f[:])
             st["xt", n] = xt
 
-        def stage_b_exit(n):
-            gx = work.tile([P, 2 * P * 4], BF16, name="gx", align_bytes=64)
-            nc.scalar.copy(out=gx[:].bitcast(F32).rearrange("p (a r u) -> p a r u", a=2, u=2),
+        def exit_x(n):
+            nc.scalar.copy(out=grouped(n)[:, 0:PW * 4].bitcast(F32).rearrange("p (a r u) -> p a r u", a=2, u=2),
                            in_=st["xt", n][:].rearrange("p a u r -> p a r u"))
-            st["gx", n] = gx
 
-        def stage_b_quant(n):
-            xq = work.tile([P, 2 * P], U32, name="xq", align_bytes=64)
-            xs = work.tile([P, 2 * P], U8, name="xs", align_bytes=64)
-            nc.vector.quantize_mx(out=xq[:].bitcast(FP8X4), scales=xs[:], in_=st["gx", n][:])
-            st["xq", n] = (xq, xs)
+        def quantise(k):
+            lo = 0 if on(k) else PW
+            hi = 2 * PW if on(k - 3) else PW
+            cod = work.tile([P, 2 * PW], U32, name="cod", align_bytes=64)
+            scl = work.tile([P, 2 * PW], U8, name="scl", align_bytes=64)
+            nc.vector.quantize_mx(out=cod[:, lo:hi].bitcast(FP8X4), scales=scl[:, lo:hi], in_=grouped(k)[:, 4 * lo:4 * hi])
+            st["cod", k] = (cod, scl)
 
-        def stage_c(n):
-            xq, xs = st["xq", n]
+        def matmul_1(n):
+            cod, scl = st["cod", n]
             for a in range(2):
                 cb = psum.tile([P, KVR], F32, name="cb", bufs=4)
-                nc.tensor.matmul_mx(out=cb[:], lhsT=xq[:, P * a:P * a + P].bitcast(FP8X4), lhsT_scale=xs[:, P * a:P * a + P],
+                nc.tensor.matmul_mx(out=cb[:], lhsT=cod[:, P * a:P * a + P].bitcast(FP8X4), lhsT_scale=scl[:, P * a:P * a + P],
                                     rhs=wcq[:].bitcast(FP8X4), rhs_scale=wcs[:], start=True, stop=True)
                 st["cb", n, a] = cb
 
-        def stage_d(n):
+        def stats(n):
             ss = small.tile([P, 2], F32, name="ss")
             for a in range(2):
                 sq = work.tile([P, KVR], BF16, name="sq")
                 nc.scalar.activation(out=sq[:], in_=st["cb", n, a][:], func=ACT.Square, accum_out=ss[:, a:a + 1])
-            rms = small.tile([P, 2], F32, name="rms")
-            nc.scalar.activation(out=rms[:], in_=ss[:], func=ACT.Sqrt, scale=1.0 / KVR, bias=eps_t[:])
-            st["rms", n] = rms
-
-        def stage_e(n):
             rstd = small.tile([P, 2], F32, name="rstd")
-            nc.vector.reciprocal(out=rstd[:], in_=st["rms", n][:])
-            cn = work.tile([P, 2, KVR], BF16, name="cn")
-            for a in range(2):
-                nc.vector.scalar_tensor_tensor(out=cn[:, a, :], in0=st["cb", n, a][:], scalar=rstd[:, a:a + 1],
-                                               in1=gain_b[:], op0=ALU.mult, op1=ALU.mult)
-            st["cn", n] = cn
+            if RSQRT:
+                nc.scalar.activation(out=rstd[:], in_=ss[:], func=ACT.Abs_reciprocal_sqrt, scale=1.0 / KVR, bias=eps_t[:])
+            else:
+                rms = small.tile([P, 2], F32, name="rms")
+                nc.scalar.activation(out=rms[:], in_=ss[:], func=ACT.Sqrt, scale=1.0 / KVR, bias=eps_t[:])
+                nc.vector.reciprocal(out=rstd[:], in_=rms[:])
+            st["rstd", n] = rstd
 
-        def stage_f(n):
+        def normalise(n, a):
+            if a == 0:
+                st["cn", n] = work.tile([P, 2, KVR], BF16, name="cn")
+            nc.vector.scalar_tensor_tensor(out=st["cn", n][:, a, :], in0=st["cb", n, a][:], scalar=st["rstd", n][:, a:a + 1],
+                                           in1=gain_b[:], op0=ALU.mult, op1=ALU.mult)
+
+        def transpose_cn(n):
             cn = st["cn", n]
             ct = psum.tile([P, 2, 4, P], BF16, name="ct")
             for a in range(2):
@@ -216,33 +239,26 @@ def tile_deepseekmultiheadattention_pb_t_kernel(tc, x, wkv_c, kv_a_norm_w, wkv_b
                     nc.tensor.transpose(ct[:, a, t, :], cn[:, a, P * t:P * t + P], ident_b[:])
             st["ct", n] = ct
 
-        def stage_g_exit(n):
-            gc = work.tile([P, 2, P, 4], BF16, name="gc", align_bytes=64)
-            nc.vector.tensor_copy(out=gc[:], in_=st["ct", n][:].rearrange("p a t r -> p a r t"))
-            st["gc", n] = gc
+        def exit_cn(n):
+            nc.vector.tensor_copy(out=grouped(n + 3)[:, PW * 4:2 * PW * 4].rearrange("p (a r t) -> p a r t", a=2, t=4),
+                                  in_=st["ct", n][:].rearrange("p a t r -> p a r t"))
 
-        def stage_g_quant(n):
-            cq = work.tile([P, 2 * P], U32, name="cq", align_bytes=64)
-            cs = work.tile([P, 2 * P], U8, name="cs", align_bytes=64)
-            nc.vector.quantize_mx(out=cq[:].bitcast(FP8X4), scales=cs[:],
-                                  in_=st["gc", n][:].rearrange("p a r t -> p (a r t)"))
-            st["cq", n] = (cq, cs)
-
-        def stage_h(n):
-            cq, cs = st["cq", n]
+        def matmul_2(n):
+            cod, scl = st["cod", n + 3]
             pv = psum.tile([P, 2, H * VD], F32, name="pv")
             pk = psum.tile([P, 2, H * NOPE], F32, name="pk")
             for a in range(2):
-                nc.tensor.matmul_mx(out=pv[:, a, :], lhsT=cq[:, P * a:P * a + P].bitcast(FP8X4), lhsT_scale=cs[:, P * a:P * a + P],
+                lo = PW + P * a
+                nc.tensor.matmul_mx(out=pv[:, a, :], lhsT=cod[:, lo:lo + P].bitcast(FP8X4), lhsT_scale=scl[:, lo:lo + P],
                                     rhs=wbvq[:].bitcast(FP8X4), rhs_scale=wbvs[:], start=True, stop=True)
-                nc.tensor.matmul_mx(out=pk[:, a, :], lhsT=cq[:, P * a:P * a + P].bitcast(FP8X4), lhsT_scale=cs[:, P * a:P * a + P],
+                nc.tensor.matmul_mx(out=pk[:, a, :], lhsT=cod[:, lo:lo + P].bitcast(FP8X4), lhsT_scale=scl[:, lo:lo + P],
                                     rhs=wbkq[:].bitcast(FP8X4), rhs_scale=wbks[:], start=True, stop=True)
             st["pv", n] = pv
             st["pk", n] = pk
 
         v_tiles = {}
 
-        def stage_i(n):
+        def exit_kv(n):
             c = n // PPC
             i0 = 2 * (n % PPC)
             if n % PPC == 0:
@@ -251,46 +267,47 @@ def tile_deepseekmultiheadattention_pb_t_kernel(tc, x, wkv_c, kv_a_norm_w, wkv_b
             nc.scalar.copy(out=vt[:, :, i0:i0 + 2, :], in_=st["pv", n][:].rearrange("p a (h d) -> p h a d", h=H))
             nc.scalar.copy(out=ks_tiles[c][:, :, i0:i0 + 2, 0:NOPE],
                            in_=st["pk", n][:].rearrange("p a (h d) -> p h a d", h=H))
-            if n % PPC == PPC - 1:
+            if c == NCH - 1:
+                lo = c * CH + i0
+                nc.sync.dma_start(out=vv[:, :, lo:lo + 2, :], in_=vt[:, :, i0:i0 + 2, :])
+                nc.sync.dma_start(out=ksv[:, :, lo:lo + 2, :], in_=ks_tiles[c][:, :, i0:i0 + 2, :])
+            elif n % PPC == PPC - 1:
                 nc.sync.dma_start(out=vv[:, :, c * CH:(c + 1) * CH, :], in_=vt[:])
                 nc.sync.dma_start(out=ksv[:, :, c * CH:(c + 1) * CH, :], in_=ks_tiles[c][:])
 
         table_start()
         prep_wc()
 
-        def on(n):
-            return 0 <= n < NPAIR
-
-        for k in range(NPAIR + 6):
-            if on(k):
-                stage_a(k)
-                if k % PPC == PPC - 1 and k // PPC + 4 < NCH:
-                    load_x(k // PPC + 4, [CH])
-            if on(k - 3):
-                stage_f(k - 3)
-            if on(k - 5):
-                stage_i(k - 5)
-            if on(k):
-                stage_b_exit(k)
+        for k in range(-1, NPAIR + 4):
+            if on(k - 1):
+                matmul_1(k - 1)
+            if on(k - 4):
+                matmul_2(k - 4)
+            if on(k - 1):
+                stats(k - 1)
+            if on(k - 4):
+                exit_kv(k - 4)
             if on(k - 2):
-                stage_e(k - 2)
+                normalise(k - 2, 0)
             if on(k - 3):
-                stage_g_exit(k - 3)
-            if on(k):
-                stage_b_quant(k)
-            if on(k - 3):
-                stage_g_quant(k - 3)
+                exit_cn(k - 3)
+            if on(k - 2):
+                normalise(k - 2, 1)
+            if on(k + 1):
+                transpose_x(k + 1)
+                if (k + 1) % PPC == PPC - 1 and (k + 1) // PPC + 4 < NCH:
+                    load_x((k + 1) // PPC + 4, [CH])
+            if on(k - 2):
+                transpose_cn(k - 2)
+            if on(k + 1):
+                exit_x(k + 1)
+            if on(k) or on(k - 3):
+                quantise(k)
             if k == 1:
                 prep_wb()
             if k == 2:
                 table_mid()
-            if on(k - 1):
-                stage_c(k - 1)
-            if on(k - 4):
-                stage_h(k - 4)
-            if on(k - 1):
-                stage_d(k - 1)
             if k == 3:
                 table_end()
-            if k >= 4 and k - 4 < NCH:
+            if k >= 4 and k - 4 < NRG:
                 rope(k - 4)

@@ -81,6 +81,9 @@ def tile_deepseekmultiheadattention_pb_t_kernel(tc, x, wkv_c, kv_a_norm_w, wkv_b
         load_x(2, [CH])
         load_x(3, [CH])
 
+        t_f = const.tile([P, TPP], F32, name="t_f")
+        nc.gpsimd.iota(t_f[:], pattern=[[1, TPP]], base=0, channel_multiplier=TPP,
+                       allow_small_or_imprecise_dtypes=True)
         ident_f = const.tile([P, P], F32, name="ident_f")
         make_identity(nc, ident_f[:])
         ident_b = const.tile([P, P], BF16, name="ident_b")
@@ -103,18 +106,22 @@ def tile_deepseekmultiheadattention_pb_t_kernel(tc, x, wkv_c, kv_a_norm_w, wkv_b
             nc.vector.quantize_mx(out=wcq[:].bitcast(FP8X4), scales=wcs[:],
                                   in_=wc_g[:].rearrange("p f t -> p (f t)"))
 
-        def prep_wb():
+        wbv_g = const.tile([P, H, VD, 4], BF16, name="wbv_g", align_bytes=64)
+        wbk_g = const.tile([P, H, NOPE, 4], BF16, name="wbk_g", align_bytes=64)
+
+        def regroup_wb():
             wbh = wb_raw[:].rearrange("p t (h c) -> p t h c", h=H)
-            wbv_g = const.tile([P, H, VD, 4], BF16, name="wbv_g", align_bytes=64)
-            wbk_g = const.tile([P, H, NOPE, 4], BF16, name="wbk_g", align_bytes=64)
-            nc.vector.tensor_copy(out=wbv_g[:], in_=wbh[:, :, :, NOPE:NOPE + VD].rearrange("p t h c -> p h c t"))
-            nc.vector.tensor_copy(out=wbk_g[:], in_=wbh[:, :, :, 0:NOPE].rearrange("p t h c -> p h c t"))
+            nc.gpsimd.tensor_scalar(out=wbv_g[:], in0=wbh[:, :, :, NOPE:NOPE + VD].rearrange("p t h c -> p h c t"),
+                                    scalar1=1.0, scalar2=0.0, op0=ALU.mult, op1=ALU.add)
+            nc.gpsimd.tensor_scalar(out=wbk_g[:], in0=wbh[:, :, :, 0:NOPE].rearrange("p t h c -> p h c t"),
+                                    scalar1=1.0, scalar2=0.0, op0=ALU.mult, op1=ALU.add)
+
+        def quantise_wb():
             nc.vector.quantize_mx(out=wbvq[:].bitcast(FP8X4), scales=wbvs[:],
                                   in_=wbv_g[:].rearrange("p h c t -> p (h c t)"))
             nc.vector.quantize_mx(out=wbkq[:].bitcast(FP8X4), scales=wbks[:],
                                   in_=wbk_g[:].rearrange("p h c t -> p (h c t)"))
 
-        t_f = const.tile([P, TPP], F32, name="t_f")
         g_b = const.tile([P, HALF], F32, name="g_b")
         turns = const.tile([P, TPP, HALF], F32, name="turns")
         whole = const.tile([P, TPP, HALF], I32, name="whole")
@@ -123,19 +130,16 @@ def tile_deepseekmultiheadattention_pb_t_kernel(tc, x, wkv_c, kv_a_norm_w, wkv_b
         TG = 8
 
         def table_start():
-            nc.gpsimd.iota(t_f[:], pattern=[[1, TPP]], base=0, channel_multiplier=TPP,
-                           allow_small_or_imprecise_dtypes=True)
             for j in range(HALF):
                 g = 10000.0 ** (-j / float(HALF)) / (2.0 * PI)
-                if j < HALF // 2:
+                if j < HALF // 4:
                     nc.vector.tensor_scalar(out=g_b[:, j:j + 1], in0=one_t[:], scalar1=g, scalar2=None, op0=ALU.mult)
                 else:
                     nc.scalar.mul(out=g_b[:, j:j + 1], in_=one_t[:], mul=g)
-            for lo in range(0, TPP, TG):
-                nc.gpsimd.tensor_tensor(out=turns[:, lo:lo + TG, :],
-                                        in0=t_f[:, lo:lo + TG].unsqueeze(2).to_broadcast([P, TG, HALF]),
-                                        in1=g_b[:].unsqueeze(1).to_broadcast([P, TG, HALF]), op=ALU.mult)
-                nc.gpsimd.tensor_scalar(out=whole[:, lo:lo + TG, :], in0=turns[:, lo:lo + TG, :],
+            nc.vector.tensor_tensor(out=turns[:], in0=t_f[:].unsqueeze(2).to_broadcast([P, TPP, HALF]),
+                                    in1=g_b[:].unsqueeze(1).to_broadcast([P, TPP, HALF]), op=ALU.mult)
+            for lo in range(0, TPP, 2 * TG):
+                nc.gpsimd.tensor_scalar(out=whole[:, lo:lo + 2 * TG, :], in0=turns[:, lo:lo + 2 * TG, :],
                                         scalar1=1.0, scalar2=0.0, op0=ALU.mult, op1=ALU.add)
 
         def table_mid():
@@ -192,8 +196,8 @@ def tile_deepseekmultiheadattention_pb_t_kernel(tc, x, wkv_c, kv_a_norm_w, wkv_b
             st["xt", n] = xt
 
         def exit_x(n):
-            nc.scalar.copy(out=grouped(n)[:, 0:PW * 4].bitcast(F32).rearrange("p (a r u) -> p a r u", a=2, u=2),
-                           in_=st["xt", n][:].rearrange("p a u r -> p a r u"))
+            nc.vector.tensor_copy(out=grouped(n)[:, 0:PW * 4].bitcast(F32).rearrange("p (a r u) -> p a r u", a=2, u=2),
+                                  in_=st["xt", n][:].rearrange("p a u r -> p a r u"))
 
         def quantise(k):
             lo = 0 if on(k) else PW
@@ -240,8 +244,8 @@ def tile_deepseekmultiheadattention_pb_t_kernel(tc, x, wkv_c, kv_a_norm_w, wkv_b
             st["ct", n] = ct
 
         def exit_cn(n):
-            nc.vector.tensor_copy(out=grouped(n + 3)[:, PW * 4:2 * PW * 4].rearrange("p (a r t) -> p a r t", a=2, t=4),
-                                  in_=st["ct", n][:].rearrange("p a t r -> p a r t"))
+            nc.scalar.copy(out=grouped(n + 3)[:, PW * 4:2 * PW * 4].rearrange("p (a r t) -> p a r t", a=2, t=4),
+                           in_=st["ct", n][:].rearrange("p a t r -> p a r t"))
 
         def matmul_2(n):
             cod, scl = st["cod", n + 3]
@@ -264,7 +268,7 @@ def tile_deepseekmultiheadattention_pb_t_kernel(tc, x, wkv_c, kv_a_norm_w, wkv_b
             if n % PPC == 0:
                 v_tiles[c] = vout.tile([P, H, CH, VD], F32, name="vt")
             vt = v_tiles[c]
-            nc.scalar.copy(out=vt[:, :, i0:i0 + 2, :], in_=st["pv", n][:].rearrange("p a (h d) -> p h a d", h=H))
+            nc.vector.tensor_copy(out=vt[:, :, i0:i0 + 2, :], in_=st["pv", n][:].rearrange("p a (h d) -> p h a d", h=H))
             nc.scalar.copy(out=ks_tiles[c][:, :, i0:i0 + 2, 0:NOPE],
                            in_=st["pk", n][:].rearrange("p a (h d) -> p h a d", h=H))
             if c == NCH - 1:
@@ -276,6 +280,7 @@ def tile_deepseekmultiheadattention_pb_t_kernel(tc, x, wkv_c, kv_a_norm_w, wkv_b
                 nc.sync.dma_start(out=ksv[:, :, c * CH:(c + 1) * CH, :], in_=ks_tiles[c][:])
 
         table_start()
+        regroup_wb()
         prep_wc()
 
         for k in range(-1, NPAIR + 4):
@@ -283,16 +288,15 @@ def tile_deepseekmultiheadattention_pb_t_kernel(tc, x, wkv_c, kv_a_norm_w, wkv_b
                 matmul_1(k - 1)
             if on(k - 4):
                 matmul_2(k - 4)
-            if on(k - 1):
-                stats(k - 1)
-            if on(k - 4):
-                exit_kv(k - 4)
-            if on(k - 2):
-                normalise(k - 2, 0)
             if on(k - 3):
                 exit_cn(k - 3)
+            if on(k - 1):
+                stats(k - 1)
             if on(k - 2):
+                normalise(k - 2, 0)
                 normalise(k - 2, 1)
+            if on(k - 4):
+                exit_kv(k - 4)
             if on(k + 1):
                 transpose_x(k + 1)
                 if (k + 1) % PPC == PPC - 1 and (k + 1) // PPC + 4 < NCH:
@@ -303,11 +307,10 @@ def tile_deepseekmultiheadattention_pb_t_kernel(tc, x, wkv_c, kv_a_norm_w, wkv_b
                 exit_x(k + 1)
             if on(k) or on(k - 3):
                 quantise(k)
-            if k == 1:
-                prep_wb()
             if k == 2:
                 table_mid()
             if k == 3:
+                quantise_wb()
                 table_end()
             if k >= 4 and k - 4 < NRG:
                 rope(k - 4)

@@ -28,8 +28,6 @@ CH = 8
 NCH = TPP // CH
 NPAIR = TPP // 2
 PPC = CH // 2
-RG = 4
-NRG = TPP // RG
 PW = 2 * P
 
 FLOPS = 2 * T * D * KVR + 2 * T * KVR * H * (NOPE + VD)
@@ -81,8 +79,10 @@ def tile_deepseekmultiheadattention_pb_t_kernel(tc, x, wkv_c, kv_a_norm_w, wkv_b
         load_x(2, [CH])
         load_x(3, [CH])
 
-        t_f = const.tile([P, TPP], F32, name="t_f")
-        nc.gpsimd.iota(t_f[:], pattern=[[1, TPP]], base=0, channel_multiplier=TPP,
+        t16 = const.tile([P, 2 * CH], F32, name="t16")
+        nc.gpsimd.iota(t16[:, 0:NCH], pattern=[[CH, NCH]], base=0, channel_multiplier=TPP,
+                       allow_small_or_imprecise_dtypes=True)
+        nc.gpsimd.iota(t16[:, NCH:NCH + CH], pattern=[[1, CH]], base=0, channel_multiplier=0,
                        allow_small_or_imprecise_dtypes=True)
         ident_f = const.tile([P, P], F32, name="ident_f")
         make_identity(nc, ident_f[:])
@@ -122,59 +122,58 @@ def tile_deepseekmultiheadattention_pb_t_kernel(tc, x, wkv_c, kv_a_norm_w, wkv_b
             nc.vector.quantize_mx(out=wbkq[:].bitcast(FP8X4), scales=wbks[:],
                                   in_=wbk_g[:].rearrange("p h c t -> p (h c t)"))
 
+        NT = NCH + CH
         g_b = const.tile([P, HALF], F32, name="g_b")
-        turns = const.tile([P, TPP, HALF], F32, name="turns")
-        whole = const.tile([P, TPP, HALF], I32, name="whole")
-        sin_t = const.tile([P, TPP, HALF], F32, name="sin_t")
-        cos_t = const.tile([P, TPP, HALF], F32, name="cos_t")
-        TG = 8
+        turns = const.tile([P, NT, HALF], F32, name="turns")
+        whole = const.tile([P, NT, HALF], I32, name="whole")
+        sin16 = const.tile([P, NT, HALF], F32, name="sin16")
+        cos16 = const.tile([P, NT, HALF], F32, name="cos16")
+        scr = const.tile([P, 1], F32, name="scr")
 
         def table_start():
             for j in range(HALF):
                 g = 10000.0 ** (-j / float(HALF)) / (2.0 * PI)
-                if j < HALF // 4:
+                if j < HALF // 2:
                     nc.vector.tensor_scalar(out=g_b[:, j:j + 1], in0=one_t[:], scalar1=g, scalar2=None, op0=ALU.mult)
                 else:
                     nc.scalar.mul(out=g_b[:, j:j + 1], in_=one_t[:], mul=g)
-            nc.vector.tensor_tensor(out=turns[:], in0=t_f[:].unsqueeze(2).to_broadcast([P, TPP, HALF]),
-                                    in1=g_b[:].unsqueeze(1).to_broadcast([P, TPP, HALF]), op=ALU.mult)
-            for lo in range(0, TPP, 2 * TG):
-                nc.gpsimd.tensor_scalar(out=whole[:, lo:lo + 2 * TG, :], in0=turns[:, lo:lo + 2 * TG, :],
-                                        scalar1=1.0, scalar2=0.0, op0=ALU.mult, op1=ALU.add)
-
-        def table_mid():
+            nc.vector.tensor_tensor(out=turns[:], in0=t16[:].unsqueeze(2).to_broadcast([P, NT, HALF]),
+                                    in1=g_b[:].unsqueeze(1).to_broadcast([P, NT, HALF]), op=ALU.mult)
+            nc.vector.tensor_copy(out=whole[:], in_=turns[:])
             nc.vector.tensor_tensor(out=turns[:], in0=turns[:], in1=whole[:], op=ALU.subtract)
 
         def table_end():
-            nc.scalar.activation(out=sin_t[:], in_=turns[:], func=ACT.Sin, scale=2.0 * PI)
-            nc.scalar.activation(out=cos_t[:], in_=turns[:], func=ACT.Sin, scale=PI)
-            for lo in range(0, TPP, TG):
-                cpart = cos_t[:, lo:lo + TG, :]
-                nc.gpsimd.tensor_tensor(out=cpart, in0=cpart, in1=cpart, op=ALU.mult)
-                nc.gpsimd.tensor_scalar(out=cpart, in0=cpart, scalar1=-2.0, scalar2=1.0, op0=ALU.mult, op1=ALU.add)
+            nc.scalar.activation(out=sin16[:], in_=turns[:], func=ACT.Sin, scale=2.0 * PI)
+            nc.scalar.activation(out=cos16[:], in_=turns[:], func=ACT.Sin, scale=PI)
+            nc.scalar.activation(out=scr[:], in_=one_t[:], func=ACT.Abs_reciprocal_sqrt)
+            nc.gpsimd.tensor_tensor(out=cos16[:], in0=cos16[:], in1=cos16[:], op=ALU.mult)
+            nc.gpsimd.tensor_scalar(out=cos16[:], in0=cos16[:], scalar1=-2.0, scalar2=1.0, op0=ALU.mult, op1=ALU.add)
 
         ks_tiles = {}
         for c in range(NCH):
             ks_tiles[c] = const.tile([P, H, CH, NOPE + ROPE], F32, name="ks%d" % c)
 
-        def rope(g):
-            lo = g * RG
-            kp = kpe_sb[:, lo:lo + RG, :].rearrange("p i (s j) -> p i s j", s=2)
-            cs = cos_t[:, lo:lo + RG, :]
-            sn = sin_t[:, lo:lo + RG, :]
-            pc = ropet.tile([P, RG, 2, HALF], F32, name="pc")
-            ps = ropet.tile([P, RG, 2, HALF], F32, name="ps")
-            nc.gpsimd.tensor_tensor(out=pc[:], in0=kp, in1=cs.unsqueeze(2).to_broadcast([P, RG, 2, HALF]), op=ALU.mult)
-            nc.gpsimd.tensor_tensor(out=ps[:], in0=kp, in1=sn.unsqueeze(2).to_broadcast([P, RG, 2, HALF]), op=ALU.mult)
-            i0 = lo % CH
-            kst = ks_tiles[lo // CH][:, :, i0:i0 + RG, :]
-            shp = [P, H, RG, HALF]
-            nc.gpsimd.tensor_tensor(out=kst[:, :, :, NOPE:NOPE + HALF],
-                                    in0=pc[:, :, 0, :].unsqueeze(1).to_broadcast(shp),
+        def rotate(out_lo, out_hi, src, cs, sn, shp):
+            pc = ropet.tile([P, CH, 2, HALF], F32, name="pc")
+            ps = ropet.tile([P, CH, 2, HALF], F32, name="ps")
+            nc.gpsimd.tensor_tensor(out=pc[:], in0=src, in1=cs, op=ALU.mult)
+            nc.gpsimd.tensor_tensor(out=ps[:], in0=src, in1=sn, op=ALU.mult)
+            nc.gpsimd.tensor_tensor(out=out_lo, in0=pc[:, :, 0, :].unsqueeze(1).to_broadcast(shp),
                                     in1=ps[:, :, 1, :].unsqueeze(1).to_broadcast(shp), op=ALU.subtract)
-            nc.gpsimd.tensor_tensor(out=kst[:, :, :, NOPE + HALF:NOPE + ROPE],
-                                    in0=ps[:, :, 0, :].unsqueeze(1).to_broadcast(shp),
+            nc.gpsimd.tensor_tensor(out=out_hi, in0=ps[:, :, 0, :].unsqueeze(1).to_broadcast(shp),
                                     in1=pc[:, :, 1, :].unsqueeze(1).to_broadcast(shp), op=ALU.add)
+
+        def rope(c):
+            full = [P, CH, 2, HALF]
+            kp = kpe_sb[:, c * CH:(c + 1) * CH, :].rearrange("p i (s j) -> p i s j", s=2)
+            y = ropet.tile([P, 1, CH, 2, HALF], F32, name="y")
+            rotate(y[:, :, :, 0, :], y[:, :, :, 1, :], kp,
+                   cos16[:, NCH:NT, :].unsqueeze(2).to_broadcast(full), sin16[:, NCH:NT, :].unsqueeze(2).to_broadcast(full),
+                   [P, 1, CH, HALF])
+            kst = ks_tiles[c]
+            rotate(kst[:, :, :, NOPE:NOPE + HALF], kst[:, :, :, NOPE + HALF:NOPE + ROPE], y[:, 0, :, :, :],
+                   cos16[:, c:c + 1, :].unsqueeze(2).to_broadcast(full), sin16[:, c:c + 1, :].unsqueeze(2).to_broadcast(full),
+                   [P, H, CH, HALF])
 
         st = {}
 
@@ -196,8 +195,8 @@ def tile_deepseekmultiheadattention_pb_t_kernel(tc, x, wkv_c, kv_a_norm_w, wkv_b
             st["xt", n] = xt
 
         def exit_x(n):
-            nc.vector.tensor_copy(out=grouped(n)[:, 0:PW * 4].bitcast(F32).rearrange("p (a r u) -> p a r u", a=2, u=2),
-                                  in_=st["xt", n][:].rearrange("p a u r -> p a r u"))
+            nc.scalar.copy(out=grouped(n)[:, 0:PW * 4].bitcast(F32).rearrange("p (a r u) -> p a r u", a=2, u=2),
+                           in_=st["xt", n][:].rearrange("p a u r -> p a r u"))
 
         def quantise(k):
             lo = 0 if on(k) else PW
@@ -244,8 +243,12 @@ def tile_deepseekmultiheadattention_pb_t_kernel(tc, x, wkv_c, kv_a_norm_w, wkv_b
             st["ct", n] = ct
 
         def exit_cn(n):
-            nc.scalar.copy(out=grouped(n + 3)[:, PW * 4:2 * PW * 4].rearrange("p (a r t) -> p a r t", a=2, t=4),
-                           in_=st["ct", n][:].rearrange("p a t r -> p a r t"))
+            dst = grouped(n + 3)[:, PW * 4:2 * PW * 4].rearrange("p (a r t) -> p a r t", a=2, t=4)
+            src = st["ct", n][:].rearrange("p a t r -> p a r t")
+            if n >= NPAIR - 2:
+                nc.scalar.copy(out=dst, in_=src)
+            else:
+                nc.vector.tensor_copy(out=dst, in_=src)
 
         def matmul_2(n):
             cod, scl = st["cod", n + 3]
@@ -268,7 +271,7 @@ def tile_deepseekmultiheadattention_pb_t_kernel(tc, x, wkv_c, kv_a_norm_w, wkv_b
             if n % PPC == 0:
                 v_tiles[c] = vout.tile([P, H, CH, VD], F32, name="vt")
             vt = v_tiles[c]
-            nc.vector.tensor_copy(out=vt[:, :, i0:i0 + 2, :], in_=st["pv", n][:].rearrange("p a (h d) -> p h a d", h=H))
+            nc.scalar.copy(out=vt[:, :, i0:i0 + 2, :], in_=st["pv", n][:].rearrange("p a (h d) -> p h a d", h=H))
             nc.scalar.copy(out=ks_tiles[c][:, :, i0:i0 + 2, 0:NOPE],
                            in_=st["pk", n][:].rearrange("p a (h d) -> p h a d", h=H))
             if c == NCH - 1:
@@ -280,7 +283,6 @@ def tile_deepseekmultiheadattention_pb_t_kernel(tc, x, wkv_c, kv_a_norm_w, wkv_b
                 nc.sync.dma_start(out=ksv[:, :, c * CH:(c + 1) * CH, :], in_=ks_tiles[c][:])
 
         table_start()
-        regroup_wb()
         prep_wc()
 
         for k in range(-1, NPAIR + 4):
@@ -288,15 +290,16 @@ def tile_deepseekmultiheadattention_pb_t_kernel(tc, x, wkv_c, kv_a_norm_w, wkv_b
                 matmul_1(k - 1)
             if on(k - 4):
                 matmul_2(k - 4)
-            if on(k - 3):
-                exit_cn(k - 3)
             if on(k - 1):
                 stats(k - 1)
-            if on(k - 2):
-                normalise(k - 2, 0)
-                normalise(k - 2, 1)
             if on(k - 4):
                 exit_kv(k - 4)
+            if on(k - 2):
+                normalise(k - 2, 0)
+            if on(k - 3):
+                exit_cn(k - 3)
+            if on(k - 2):
+                normalise(k - 2, 1)
             if on(k + 1):
                 transpose_x(k + 1)
                 if (k + 1) % PPC == PPC - 1 and (k + 1) // PPC + 4 < NCH:
@@ -307,10 +310,10 @@ def tile_deepseekmultiheadattention_pb_t_kernel(tc, x, wkv_c, kv_a_norm_w, wkv_b
                 exit_x(k + 1)
             if on(k) or on(k - 3):
                 quantise(k)
-            if k == 2:
-                table_mid()
+            if k == -1:
+                table_end()
+                regroup_wb()
             if k == 3:
                 quantise_wb()
-                table_end()
-            if k >= 4 and k - 4 < NRG:
-                rope(k - 4)
+            if 0 <= k < NCH:
+                rope(k)

@@ -29,6 +29,8 @@ NCH = TPP // CH
 NPAIR = TPP // 2
 PPC = CH // 2
 PW = 2 * P
+RG = 4
+NRG = TPP // RG
 
 FLOPS = 2 * T * D * KVR + 2 * T * KVR * H * (NOPE + VD)
 MANUAL = True
@@ -153,27 +155,26 @@ def tile_deepseekmultiheadattention_pb_t_kernel(tc, x, wkv_c, kv_a_norm_w, wkv_b
         for c in range(NCH):
             ks_tiles[c] = const.tile([P, H, CH, NOPE + ROPE], F32, name="ks%d" % c)
 
-        def rotate(out_lo, out_hi, src, cs, sn, shp):
-            pc = ropet.tile([P, CH, 2, HALF], F32, name="pc")
-            ps = ropet.tile([P, CH, 2, HALF], F32, name="ps")
+        def rotate(out_lo, out_hi, src, cs, sn):
+            pc = ropet.tile([P, RG, 2, HALF], F32, name="pc")
+            ps = ropet.tile([P, RG, 2, HALF], F32, name="ps")
             nc.gpsimd.tensor_tensor(out=pc[:], in0=src, in1=cs, op=ALU.mult)
             nc.gpsimd.tensor_tensor(out=ps[:], in0=src, in1=sn, op=ALU.mult)
-            nc.gpsimd.tensor_tensor(out=out_lo, in0=pc[:, :, 0, :].unsqueeze(1).to_broadcast(shp),
-                                    in1=ps[:, :, 1, :].unsqueeze(1).to_broadcast(shp), op=ALU.subtract)
-            nc.gpsimd.tensor_tensor(out=out_hi, in0=ps[:, :, 0, :].unsqueeze(1).to_broadcast(shp),
-                                    in1=pc[:, :, 1, :].unsqueeze(1).to_broadcast(shp), op=ALU.add)
+            nc.gpsimd.tensor_tensor(out=out_lo, in0=pc[:, :, 0, :], in1=ps[:, :, 1, :], op=ALU.subtract)
+            nc.gpsimd.tensor_tensor(out=out_hi, in0=ps[:, :, 0, :], in1=pc[:, :, 1, :], op=ALU.add)
 
-        def rope(c):
-            full = [P, CH, 2, HALF]
-            kp = kpe_sb[:, c * CH:(c + 1) * CH, :].rearrange("p i (s j) -> p i s j", s=2)
-            y = ropet.tile([P, 1, CH, 2, HALF], F32, name="y")
-            rotate(y[:, :, :, 0, :], y[:, :, :, 1, :], kp,
-                   cos16[:, NCH:NT, :].unsqueeze(2).to_broadcast(full), sin16[:, NCH:NT, :].unsqueeze(2).to_broadcast(full),
-                   [P, 1, CH, HALF])
-            kst = ks_tiles[c]
-            rotate(kst[:, :, :, NOPE:NOPE + HALF], kst[:, :, :, NOPE + HALF:NOPE + ROPE], y[:, 0, :, :, :],
-                   cos16[:, c:c + 1, :].unsqueeze(2).to_broadcast(full), sin16[:, c:c + 1, :].unsqueeze(2).to_broadcast(full),
-                   [P, H, CH, HALF])
+        def rope(g):
+            full = [P, RG, 2, HALF]
+            c = g * RG // CH
+            b0 = g * RG % CH
+            kp = kpe_sb[:, g * RG:(g + 1) * RG, :].rearrange("p i (s j) -> p i s j", s=2)
+            y = ropet.tile([P, RG, 2, HALF], F32, name="y")
+            rotate(y[:, :, 0, :], y[:, :, 1, :], kp,
+                   cos16[:, NCH + b0:NCH + b0 + RG, :].unsqueeze(2).to_broadcast(full),
+                   sin16[:, NCH + b0:NCH + b0 + RG, :].unsqueeze(2).to_broadcast(full))
+            kst = ks_tiles[c][:, 0, b0:b0 + RG, :]
+            rotate(kst[:, :, NOPE:NOPE + HALF], kst[:, :, NOPE + HALF:NOPE + ROPE], y[:],
+                   cos16[:, c:c + 1, :].unsqueeze(2).to_broadcast(full), sin16[:, c:c + 1, :].unsqueeze(2).to_broadcast(full))
 
         st = {}
 
@@ -265,6 +266,14 @@ def tile_deepseekmultiheadattention_pb_t_kernel(tc, x, wkv_c, kv_a_norm_w, wkv_b
 
         v_tiles = {}
 
+        def store(c, i0, n):
+            lo = c * CH + i0
+            kst = ks_tiles[c]
+            nc.sync.dma_start(out=vv[:, :, lo:lo + n, :], in_=v_tiles[c][:, :, i0:i0 + n, :])
+            nc.sync.dma_start(out=ksv[:, 0, lo:lo + n, :], in_=kst[:, 0, i0:i0 + n, :])
+            nc.sync.dma_start(out=ksv[:, 1, lo:lo + n, 0:NOPE], in_=kst[:, 1, i0:i0 + n, 0:NOPE])
+            nc.sync.dma_start(out=ksv[:, 1, lo:lo + n, NOPE:NOPE + ROPE], in_=kst[:, 0, i0:i0 + n, NOPE:NOPE + ROPE])
+
         def exit_kv(n):
             c = n // PPC
             i0 = 2 * (n % PPC)
@@ -275,12 +284,9 @@ def tile_deepseekmultiheadattention_pb_t_kernel(tc, x, wkv_c, kv_a_norm_w, wkv_b
             nc.scalar.copy(out=ks_tiles[c][:, :, i0:i0 + 2, 0:NOPE],
                            in_=st["pk", n][:].rearrange("p a (h d) -> p h a d", h=H))
             if c == NCH - 1:
-                lo = c * CH + i0
-                nc.sync.dma_start(out=vv[:, :, lo:lo + 2, :], in_=vt[:, :, i0:i0 + 2, :])
-                nc.sync.dma_start(out=ksv[:, :, lo:lo + 2, :], in_=ks_tiles[c][:, :, i0:i0 + 2, :])
+                store(c, i0, 2)
             elif n % PPC == PPC - 1:
-                nc.sync.dma_start(out=vv[:, :, c * CH:(c + 1) * CH, :], in_=vt[:])
-                nc.sync.dma_start(out=ksv[:, :, c * CH:(c + 1) * CH, :], in_=ks_tiles[c][:])
+                store(c, 0, CH)
 
         table_start()
         prep_wc()
@@ -315,5 +321,5 @@ def tile_deepseekmultiheadattention_pb_t_kernel(tc, x, wkv_c, kv_a_norm_w, wkv_b
                 regroup_wb()
             if k == 3:
                 quantise_wb()
-            if 0 <= k < NCH:
+            if 0 <= k < NRG:
                 rope(k)

@@ -294,11 +294,14 @@ def tile_deepseekmultiheadattention_pb_t_kernel(tc, x, wkv_c, kv_a_norm_w, wkv_b
         for k in range(-1, NPAIR + 4):
             if on(k - 1):
                 matmul_1(k - 1)
+                stats(k - 1)
+            if on(k + 1):
+                transpose_x(k + 1)
+                if (k + 1) % PPC == PPC - 1 and (k + 1) // PPC + 4 < NCH:
+                    load_x((k + 1) // PPC + 4, [CH])
+                exit_x(k + 1)
             if on(k - 4):
                 matmul_2(k - 4)
-            if on(k - 1):
-                stats(k - 1)
-            if on(k - 4):
                 exit_kv(k - 4)
             if on(k - 2):
                 normalise(k - 2, 0)
@@ -306,14 +309,7 @@ def tile_deepseekmultiheadattention_pb_t_kernel(tc, x, wkv_c, kv_a_norm_w, wkv_b
                 exit_cn(k - 3)
             if on(k - 2):
                 normalise(k - 2, 1)
-            if on(k + 1):
-                transpose_x(k + 1)
-                if (k + 1) % PPC == PPC - 1 and (k + 1) // PPC + 4 < NCH:
-                    load_x((k + 1) // PPC + 4, [CH])
-            if on(k - 2):
                 transpose_cn(k - 2)
-            if on(k + 1):
-                exit_x(k + 1)
             if on(k) or on(k - 3):
                 quantise(k)
             if k == -1:

@@ -246,10 +246,7 @@ def tile_deepseekmultiheadattention_pb_t_kernel(tc, x, wkv_c, kv_a_norm_w, wkv_b
         def exit_cn(n):
             dst = grouped(n + 3)[:, PW * 4:2 * PW * 4].rearrange("p (a r t) -> p a r t", a=2, t=4)
             src = st["ct", n][:].rearrange("p a t r -> p a r t")
-            if n >= NPAIR - 2:
-                nc.scalar.copy(out=dst, in_=src)
-            else:
-                nc.vector.tensor_copy(out=dst, in_=src)
+            nc.scalar.copy(out=dst, in_=src)
 
         def matmul_2(n):
             cod, scl = st["cod", n + 3]
@@ -280,9 +277,9 @@ def tile_deepseekmultiheadattention_pb_t_kernel(tc, x, wkv_c, kv_a_norm_w, wkv_b
             if n % PPC == 0:
                 v_tiles[c] = vout.tile([P, H, CH, VD], F32, name="vt")
             vt = v_tiles[c]
-            nc.scalar.copy(out=vt[:, :, i0:i0 + 2, :], in_=st["pv", n][:].rearrange("p a (h d) -> p h a d", h=H))
-            nc.scalar.copy(out=ks_tiles[c][:, :, i0:i0 + 2, 0:NOPE],
-                           in_=st["pk", n][:].rearrange("p a (h d) -> p h a d", h=H))
+            nc.vector.tensor_copy(out=vt[:, :, i0:i0 + 2, :], in_=st["pv", n][:].rearrange("p a (h d) -> p h a d", h=H))
+            nc.vector.tensor_copy(out=ks_tiles[c][:, :, i0:i0 + 2, 0:NOPE],
+                                  in_=st["pk", n][:].rearrange("p a (h d) -> p h a d", h=H))
             if c == NCH - 1:
                 store(c, i0, 2)
             elif n % PPC == PPC - 1:
@@ -291,25 +288,28 @@ def tile_deepseekmultiheadattention_pb_t_kernel(tc, x, wkv_c, kv_a_norm_w, wkv_b
         table_start()
         prep_wc()
 
-        for k in range(-1, NPAIR + 4):
+        for k in range(-1, NPAIR + 5):
             if on(k - 1):
                 matmul_1(k - 1)
+            if on(k - 5):
+                exit_kv(k - 5)
+            if on(k - 4):
+                matmul_2(k - 4)
+            if on(k - 3):
+                exit_cn(k - 3)
+            if on(k - 1):
                 stats(k - 1)
+            if on(k - 2):
+                normalise(k - 2, 0)
+                normalise(k - 2, 1)
             if on(k + 1):
                 transpose_x(k + 1)
                 if (k + 1) % PPC == PPC - 1 and (k + 1) // PPC + 4 < NCH:
                     load_x((k + 1) // PPC + 4, [CH])
-                exit_x(k + 1)
-            if on(k - 4):
-                matmul_2(k - 4)
-                exit_kv(k - 4)
             if on(k - 2):
-                normalise(k - 2, 0)
-            if on(k - 3):
-                exit_cn(k - 3)
-            if on(k - 2):
-                normalise(k - 2, 1)
                 transpose_cn(k - 2)
+            if on(k + 1):
+                exit_x(k + 1)
             if on(k) or on(k - 3):
                 quantise(k)
             if k == -1:

@@ -13,6 +13,7 @@ ALU = mybir.AluOpType
 ACT = mybir.ActivationFunctionType
 
 P = 128
+PACK = 4
 T = 8192
 D = 512
 KVR = 512
@@ -20,7 +21,7 @@ H = 2
 NOPE = 64
 VD = 128
 ROPE = 64
-HALF = 32
+HALF = ROPE // 2
 EPS = 1.1920928955078125e-07
 PI = 3.141592653589793
 TPP = T // P
@@ -30,61 +31,60 @@ NPAIR = TPP // 2
 PPC = CH // 2
 PW = 2 * P
 RG = 4
-NRG = TPP // RG
+X_BUFS = 4
 
 FLOPS = 2 * T * D * KVR + 2 * T * KVR * H * (NOPE + VD)
-MANUAL = True
-RSQRT = True
 
 
 def tile_deepseekmultiheadattention_pb_t_kernel(tc, x, wkv_c, kv_a_norm_w, wkv_b, k_pe, out_0, out_1):
     nc = tc.nc
-    xv = x.flatten_outer_dims().rearrange("(p i) k -> p i k", i=TPP)
-    kpv = k_pe.flatten_outer_dims().rearrange("(p i) k -> p i k", i=TPP)
-    ksv = out_0.rearrange("o h (p i) d -> p (o h) i d", i=TPP)
-    vv = out_1.rearrange("o h (p i) d -> p (o h) i d", i=TPP)
+    x_view = x.flatten_outer_dims().rearrange("(p i) k -> p i k", i=TPP)
+    kpe_view = k_pe.flatten_outer_dims().rearrange("(p i) d -> p i d", i=TPP)
+    ks_view = out_0.rearrange("o h (p i) d -> p (o h) i d", i=TPP)
+    v_view = out_1.rearrange("o h (p i) d -> p (o h) i d", i=TPP)
 
     with ExitStack() as ctx:
         const = ctx.enter_context(tc.tile_pool(name="const", bufs=1))
-        xin = ctx.enter_context(tc.tile_pool(name="xin", bufs=4))
+        xin = ctx.enter_context(tc.tile_pool(name="xin", bufs=X_BUFS))
         work = ctx.enter_context(tc.tile_pool(name="work", bufs=3))
         small = ctx.enter_context(tc.tile_pool(name="small", bufs=4))
         vout = ctx.enter_context(tc.tile_pool(name="vout", bufs=3))
-        ropet = ctx.enter_context(tc.tile_pool(name="ropet", bufs=2))
+        turn = ctx.enter_context(tc.tile_pool(name="turn", bufs=2))
         psum = ctx.enter_context(tc.psum_pool(name="psum", bufs=1))
-        if MANUAL:
-            ctx.enter_context(tc.manual_schedule())
+        ctx.enter_context(tc.manual_schedule())
 
-        x_tiles = {}
+        x_chunks = {}
 
-        def load_x(c, pieces):
+        def load_x(chunk, pieces):
             xc = xin.tile([P, CH, D], BF16, name="xc")
             lo = 0
-            for n in pieces:
-                nc.sync.dma_start(out=xc[:, lo:lo + n, :], in_=xv[:, c * CH + lo:c * CH + lo + n, :])
-                lo += n
-            x_tiles[c] = xc
+            for count in pieces:
+                nc.sync.dma_start(out=xc[:, lo:lo + count, :],
+                                  in_=x_view[:, chunk * CH + lo:chunk * CH + lo + count, :])
+                lo += count
+            x_chunks[chunk] = xc
 
-        wc_raw = const.tile([P, 4, KVR], BF16, name="wc_raw")
-        wb_raw = const.tile([P, 4, H * (NOPE + VD)], BF16, name="wb_raw")
-        gain_b = const.tile([P, KVR], BF16, name="gain_b")
-        kpe_sb = const.tile([P, TPP, ROPE], BF16, name="kpe_sb")
+        wc_raw = const.tile([P, PACK, KVR], BF16, name="wc_raw")
+        wb_raw = const.tile([P, PACK, H * (NOPE + VD)], BF16, name="wb_raw")
+        gain = const.tile([P, KVR], BF16, name="gain")
+        kpe = const.tile([P, TPP, ROPE], BF16, name="kpe")
 
-        load_x(0, [2, 6])
+        load_x(0, [2, CH - 2])
         for u in range(2):
             nc.scalar.dma_start(out=wc_raw[:, 2 * u:2 * u + 2, :],
                                 in_=wkv_c[256 * u:256 * u + 256, :].rearrange("(p e) f -> p e f", e=2))
-        nc.scalar.dma_start(out=gain_b[:], in_=kv_a_norm_w.partition_broadcast(P))
-        nc.scalar.dma_start(out=wb_raw[:], in_=wkv_b.rearrange("(t p) c -> p t c", p=P))
+        nc.scalar.dma_start(out=gain[:], in_=kv_a_norm_w.partition_broadcast(P))
+        nc.sync.dma_start(out=wb_raw[:], in_=wkv_b.rearrange("(t p) w -> p t w", p=P))
         load_x(1, [CH])
-        nc.sync.dma_start(out=kpe_sb[:], in_=kpv)
-        load_x(2, [CH])
-        load_x(3, [CH])
+        nc.sync.dma_start(out=kpe[:], in_=kpe_view)
+        for chunk in range(2, X_BUFS):
+            load_x(chunk, [CH])
 
-        t16 = const.tile([P, 2 * CH], F32, name="t16")
-        nc.gpsimd.iota(t16[:, 0:NCH], pattern=[[CH, NCH]], base=0, channel_multiplier=TPP,
+        NPOS = NCH + CH
+        pos = const.tile([P, NPOS], F32, name="pos")
+        nc.gpsimd.iota(pos[:, 0:NCH], pattern=[[CH, NCH]], base=0, channel_multiplier=TPP,
                        allow_small_or_imprecise_dtypes=True)
-        nc.gpsimd.iota(t16[:, NCH:NCH + CH], pattern=[[1, CH]], base=0, channel_multiplier=0,
+        nc.gpsimd.iota(pos[:, NCH:NPOS], pattern=[[1, CH]], base=0, channel_multiplier=0,
                        allow_small_or_imprecise_dtypes=True)
         ident_f = const.tile([P, P], F32, name="ident_f")
         make_identity(nc, ident_f[:])
@@ -95,227 +95,225 @@ def tile_deepseekmultiheadattention_pb_t_kernel(tc, x, wkv_c, kv_a_norm_w, wkv_b
         one_t = const.tile([P, 1], F32, name="one_t")
         nc.vector.memset(one_t[:], 1.0)
 
-        wcq = const.tile([P, KVR], U32, name="wcq", align_bytes=64)
-        wcs = const.tile([P, KVR], U8, name="wcs", align_bytes=64)
-        wbvq = const.tile([P, H * VD], U32, name="wbvq", align_bytes=64)
-        wbvs = const.tile([P, H * VD], U8, name="wbvs", align_bytes=64)
-        wbkq = const.tile([P, H * NOPE], U32, name="wbkq", align_bytes=64)
-        wbks = const.tile([P, H * NOPE], U8, name="wbks", align_bytes=64)
+        freq = const.tile([P, HALF], F32, name="freq")
+        turns = const.tile([P, NPOS, HALF], F32, name="turns")
+        whole = const.tile([P, NPOS, HALF], I32, name="whole")
+        sin_t = const.tile([P, NPOS, HALF], F32, name="sin_t")
+        cos_t = const.tile([P, NPOS, HALF], F32, name="cos_t")
+        unused = const.tile([P, 1], F32, name="unused")
 
-        def prep_wc():
-            wc_g = const.tile([P, KVR, 4], BF16, name="wc_g", align_bytes=64)
-            nc.vector.tensor_copy(out=wc_g[:], in_=wc_raw[:].rearrange("p t f -> p f t"))
-            nc.vector.quantize_mx(out=wcq[:].bitcast(FP8X4), scales=wcs[:],
-                                  in_=wc_g[:].rearrange("p f t -> p (f t)"))
-
-        wbv_g = const.tile([P, H, VD, 4], BF16, name="wbv_g", align_bytes=64)
-        wbk_g = const.tile([P, H, NOPE, 4], BF16, name="wbk_g", align_bytes=64)
-
-        def regroup_wb():
-            wbh = wb_raw[:].rearrange("p t (h c) -> p t h c", h=H)
-            nc.gpsimd.tensor_scalar(out=wbv_g[:], in0=wbh[:, :, :, NOPE:NOPE + VD].rearrange("p t h c -> p h c t"),
-                                    scalar1=1.0, scalar2=0.0, op0=ALU.mult, op1=ALU.add)
-            nc.gpsimd.tensor_scalar(out=wbk_g[:], in0=wbh[:, :, :, 0:NOPE].rearrange("p t h c -> p h c t"),
-                                    scalar1=1.0, scalar2=0.0, op0=ALU.mult, op1=ALU.add)
-
-        def quantise_wb():
-            nc.vector.quantize_mx(out=wbvq[:].bitcast(FP8X4), scales=wbvs[:],
-                                  in_=wbv_g[:].rearrange("p h c t -> p (h c t)"))
-            nc.vector.quantize_mx(out=wbkq[:].bitcast(FP8X4), scales=wbks[:],
-                                  in_=wbk_g[:].rearrange("p h c t -> p (h c t)"))
-
-        NT = NCH + CH
-        g_b = const.tile([P, HALF], F32, name="g_b")
-        turns = const.tile([P, NT, HALF], F32, name="turns")
-        whole = const.tile([P, NT, HALF], I32, name="whole")
-        sin16 = const.tile([P, NT, HALF], F32, name="sin16")
-        cos16 = const.tile([P, NT, HALF], F32, name="cos16")
-        scr = const.tile([P, 1], F32, name="scr")
-
-        def table_start():
+        def reduce_angles():
             for j in range(HALF):
-                g = 10000.0 ** (-j / float(HALF)) / (2.0 * PI)
+                turns_a_position = 10000.0 ** (-j / float(HALF)) / (2.0 * PI)
                 if j < HALF // 2:
-                    nc.vector.tensor_scalar(out=g_b[:, j:j + 1], in0=one_t[:], scalar1=g, scalar2=None, op0=ALU.mult)
+                    nc.vector.tensor_scalar(out=freq[:, j:j + 1], in0=one_t[:], scalar1=turns_a_position, scalar2=None,
+                                            op0=ALU.mult)
                 else:
-                    nc.scalar.mul(out=g_b[:, j:j + 1], in_=one_t[:], mul=g)
-            nc.vector.tensor_tensor(out=turns[:], in0=t16[:].unsqueeze(2).to_broadcast([P, NT, HALF]),
-                                    in1=g_b[:].unsqueeze(1).to_broadcast([P, NT, HALF]), op=ALU.mult)
+                    nc.scalar.mul(out=freq[:, j:j + 1], in_=one_t[:], mul=turns_a_position)
+            nc.vector.tensor_tensor(out=turns[:], in0=pos[:].unsqueeze(2).to_broadcast([P, NPOS, HALF]),
+                                    in1=freq[:].unsqueeze(1).to_broadcast([P, NPOS, HALF]), op=ALU.mult)
             nc.vector.tensor_copy(out=whole[:], in_=turns[:])
             nc.vector.tensor_tensor(out=turns[:], in0=turns[:], in1=whole[:], op=ALU.subtract)
 
-        def table_end():
-            nc.scalar.activation(out=sin16[:], in_=turns[:], func=ACT.Sin, scale=2.0 * PI)
-            nc.scalar.activation(out=cos16[:], in_=turns[:], func=ACT.Sin, scale=PI)
-            nc.scalar.activation(out=scr[:], in_=one_t[:], func=ACT.Abs_reciprocal_sqrt)
-            nc.gpsimd.tensor_tensor(out=cos16[:], in0=cos16[:], in1=cos16[:], op=ALU.mult)
-            nc.gpsimd.tensor_scalar(out=cos16[:], in0=cos16[:], scalar1=-2.0, scalar2=1.0, op0=ALU.mult, op1=ALU.add)
+        def make_tables():
+            nc.scalar.activation(out=sin_t[:], in_=turns[:], func=ACT.Sin, scale=2.0 * PI)
+            nc.scalar.activation(out=cos_t[:], in_=turns[:], func=ACT.Sin, scale=PI)
+            nc.scalar.activation(out=unused[:], in_=one_t[:], func=ACT.Abs_reciprocal_sqrt)
+            nc.gpsimd.tensor_tensor(out=cos_t[:], in0=cos_t[:], in1=cos_t[:], op=ALU.mult)
+            nc.gpsimd.tensor_scalar(out=cos_t[:], in0=cos_t[:], scalar1=-2.0, scalar2=1.0, op0=ALU.mult, op1=ALU.add)
 
-        ks_tiles = {}
-        for c in range(NCH):
-            ks_tiles[c] = const.tile([P, H, CH, NOPE + ROPE], F32, name="ks%d" % c)
+        wc_words = const.tile([P, KVR], U32, name="wc_words", align_bytes=64)
+        wc_scales = const.tile([P, KVR], U8, name="wc_scales", align_bytes=64)
+        wv_words = const.tile([P, H * VD], U32, name="wv_words", align_bytes=64)
+        wv_scales = const.tile([P, H * VD], U8, name="wv_scales", align_bytes=64)
+        wk_words = const.tile([P, H * NOPE], U32, name="wk_words", align_bytes=64)
+        wk_scales = const.tile([P, H * NOPE], U8, name="wk_scales", align_bytes=64)
 
-        def rotate(out_lo, out_hi, src, cs, sn):
-            pc = ropet.tile([P, RG, 2, HALF], F32, name="pc")
-            ps = ropet.tile([P, RG, 2, HALF], F32, name="ps")
-            nc.gpsimd.tensor_tensor(out=pc[:], in0=src, in1=cs, op=ALU.mult)
-            nc.gpsimd.tensor_tensor(out=ps[:], in0=src, in1=sn, op=ALU.mult)
-            nc.gpsimd.tensor_tensor(out=out_lo, in0=pc[:, :, 0, :], in1=ps[:, :, 1, :], op=ALU.subtract)
-            nc.gpsimd.tensor_tensor(out=out_hi, in0=ps[:, :, 0, :], in1=pc[:, :, 1, :], op=ALU.add)
+        def quantise_wkv_c():
+            wc_grouped = const.tile([P, KVR, PACK], BF16, name="wc_grouped", align_bytes=64)
+            nc.vector.tensor_copy(out=wc_grouped[:], in_=wc_raw[:].rearrange("p t f -> p f t"))
+            nc.vector.quantize_mx(out=wc_words[:].bitcast(FP8X4), scales=wc_scales[:],
+                                  in_=wc_grouped[:].rearrange("p f t -> p (f t)"))
 
-        def rope(g):
-            full = [P, RG, 2, HALF]
-            c = g * RG // CH
-            b0 = g * RG % CH
-            kp = kpe_sb[:, g * RG:(g + 1) * RG, :].rearrange("p i (s j) -> p i s j", s=2)
-            y = ropet.tile([P, RG, 2, HALF], F32, name="y")
-            rotate(y[:, :, 0, :], y[:, :, 1, :], kp,
-                   cos16[:, NCH + b0:NCH + b0 + RG, :].unsqueeze(2).to_broadcast(full),
-                   sin16[:, NCH + b0:NCH + b0 + RG, :].unsqueeze(2).to_broadcast(full))
-            kst = ks_tiles[c][:, 0, b0:b0 + RG, :]
-            rotate(kst[:, :, NOPE:NOPE + HALF], kst[:, :, NOPE + HALF:NOPE + ROPE], y[:],
-                   cos16[:, c:c + 1, :].unsqueeze(2).to_broadcast(full), sin16[:, c:c + 1, :].unsqueeze(2).to_broadcast(full))
+        def quantise_wkv_b():
+            by_head = wb_raw[:].rearrange("p t (h d) -> p t h d", h=H)
+            wv_grouped = const.tile([P, H, VD, PACK], BF16, name="wv_grouped", align_bytes=64)
+            wk_grouped = const.tile([P, H, NOPE, PACK], BF16, name="wk_grouped", align_bytes=64)
+            nc.vector.tensor_copy(out=wv_grouped[:], in_=by_head[:, :, :, NOPE:NOPE + VD].rearrange("p t h d -> p h d t"))
+            nc.vector.tensor_copy(out=wk_grouped[:], in_=by_head[:, :, :, 0:NOPE].rearrange("p t h d -> p h d t"))
+            nc.vector.quantize_mx(out=wv_words[:].bitcast(FP8X4), scales=wv_scales[:],
+                                  in_=wv_grouped[:].rearrange("p h d t -> p (h d t)"))
+            nc.vector.quantize_mx(out=wk_words[:].bitcast(FP8X4), scales=wk_scales[:],
+                                  in_=wk_grouped[:].rearrange("p h d t -> p (h d t)"))
 
-        st = {}
+        ks_chunks = {}
+        for chunk in range(NCH):
+            ks_chunks[chunk] = const.tile([P, H, CH, NOPE + ROPE], F32, name="ks%d" % chunk)
+
+        def rotate(out_lo, out_hi, src, cos_a, sin_a):
+            by_cos = turn.tile([P, RG, 2, HALF], F32, name="by_cos")
+            by_sin = turn.tile([P, RG, 2, HALF], F32, name="by_sin")
+            nc.gpsimd.tensor_tensor(out=by_cos[:], in0=src, in1=cos_a, op=ALU.mult)
+            nc.gpsimd.tensor_tensor(out=by_sin[:], in0=src, in1=sin_a, op=ALU.mult)
+            nc.gpsimd.tensor_tensor(out=out_lo, in0=by_cos[:, :, 0, :], in1=by_sin[:, :, 1, :], op=ALU.subtract)
+            nc.gpsimd.tensor_tensor(out=out_hi, in0=by_sin[:, :, 0, :], in1=by_cos[:, :, 1, :], op=ALU.add)
+
+        def rotate_keys(g):
+            shape = [P, RG, 2, HALF]
+            chunk = g * RG // CH
+            b = g * RG % CH
+            once = turn.tile([P, RG, 2, HALF], F32, name="once")
+            rotate(once[:, :, 0, :], once[:, :, 1, :],
+                   kpe[:, g * RG:(g + 1) * RG, :].rearrange("p i (s j) -> p i s j", s=2),
+                   cos_t[:, NCH + b:NCH + b + RG, :].unsqueeze(2).to_broadcast(shape),
+                   sin_t[:, NCH + b:NCH + b + RG, :].unsqueeze(2).to_broadcast(shape))
+            rows = ks_chunks[chunk][:, 0, b:b + RG, :]
+            rotate(rows[:, :, NOPE:NOPE + HALF], rows[:, :, NOPE + HALF:NOPE + ROPE], once[:],
+                   cos_t[:, chunk:chunk + 1, :].unsqueeze(2).to_broadcast(shape),
+                   sin_t[:, chunk:chunk + 1, :].unsqueeze(2).to_broadcast(shape))
+
+        live = {}
 
         def on(n):
             return 0 <= n < NPAIR
 
-        def grouped(k):
-            if ("grp", k) not in st:
-                st["grp", k] = work.tile([P, 2 * PW * 4], BF16, name="grp", align_bytes=64)
-            return st["grp", k]
+        def grouped(period):
+            if ("grouped", period) not in live:
+                live["grouped", period] = work.tile([P, 2 * PW * PACK], BF16, name="grouped", align_bytes=64)
+            return live["grouped", period]
 
         def transpose_x(n):
-            xc = x_tiles[n // PPC]
+            xc = x_chunks[n // PPC]
             xt = psum.tile([P, 2, 2, P], F32, name="xt")
             for a in range(2):
-                xw = xc[:, 2 * (n % PPC) + a, :].bitcast(F32)
+                as_f32 = xc[:, 2 * (n % PPC) + a, :].bitcast(F32)
                 for u in range(2):
-                    nc.tensor.transpose(xt[:, a, u, :], xw[:, P * u:P * u + P], ident_f[:])
-            st["xt", n] = xt
+                    nc.tensor.transpose(xt[:, a, u, :], as_f32[:, P * u:P * u + P], ident_f[:])
+            live["xt", n] = xt
 
-        def exit_x(n):
-            nc.scalar.copy(out=grouped(n)[:, 0:PW * 4].bitcast(F32).rearrange("p (a r u) -> p a r u", a=2, u=2),
-                           in_=st["xt", n][:].rearrange("p a u r -> p a r u"))
+        def copy_x(n):
+            nc.scalar.copy(out=grouped(n)[:, 0:PW * PACK].bitcast(F32).rearrange("p (a r u) -> p a r u", a=2, u=2),
+                           in_=live["xt", n][:].rearrange("p a u r -> p a r u"))
 
-        def quantise(k):
-            lo = 0 if on(k) else PW
-            hi = 2 * PW if on(k - 3) else PW
-            cod = work.tile([P, 2 * PW], U32, name="cod", align_bytes=64)
-            scl = work.tile([P, 2 * PW], U8, name="scl", align_bytes=64)
-            nc.vector.quantize_mx(out=cod[:, lo:hi].bitcast(FP8X4), scales=scl[:, lo:hi], in_=grouped(k)[:, 4 * lo:4 * hi])
-            st["cod", k] = (cod, scl)
+        def quantise(period):
+            lo = 0 if on(period) else PW
+            hi = 2 * PW if on(period - 3) else PW
+            words = work.tile([P, 2 * PW], U32, name="words", align_bytes=64)
+            scales = work.tile([P, 2 * PW], U8, name="scales", align_bytes=64)
+            nc.vector.quantize_mx(out=words[:, lo:hi].bitcast(FP8X4), scales=scales[:, lo:hi],
+                                  in_=grouped(period)[:, PACK * lo:PACK * hi])
+            live["quantised", period] = (words, scales)
 
         def matmul_1(n):
-            cod, scl = st["cod", n]
+            words, scales = live["quantised", n]
             for a in range(2):
-                cb = psum.tile([P, KVR], F32, name="cb", bufs=4)
-                nc.tensor.matmul_mx(out=cb[:], lhsT=cod[:, P * a:P * a + P].bitcast(FP8X4), lhsT_scale=scl[:, P * a:P * a + P],
-                                    rhs=wcq[:].bitcast(FP8X4), rhs_scale=wcs[:], start=True, stop=True)
-                st["cb", n, a] = cb
+                c_ps = psum.tile([P, KVR], F32, name="c_ps", bufs=4)
+                nc.tensor.matmul_mx(out=c_ps[:], lhsT=words[:, P * a:P * a + P].bitcast(FP8X4),
+                                    lhsT_scale=scales[:, P * a:P * a + P],
+                                    rhs=wc_words[:].bitcast(FP8X4), rhs_scale=wc_scales[:], start=True, stop=True)
+                live["c", n, a] = c_ps
 
-        def stats(n):
-            ss = small.tile([P, 2], F32, name="ss")
+        def statistics(n):
+            sums = small.tile([P, 2], F32, name="sums")
             for a in range(2):
-                sq = work.tile([P, KVR], BF16, name="sq")
-                nc.scalar.activation(out=sq[:], in_=st["cb", n, a][:], func=ACT.Square, accum_out=ss[:, a:a + 1])
+                squares = work.tile([P, KVR], BF16, name="squares")
+                nc.scalar.activation(out=squares[:], in_=live["c", n, a][:], func=ACT.Square, accum_out=sums[:, a:a + 1])
             rstd = small.tile([P, 2], F32, name="rstd")
-            if RSQRT:
-                nc.scalar.activation(out=rstd[:], in_=ss[:], func=ACT.Abs_reciprocal_sqrt, scale=1.0 / KVR, bias=eps_t[:])
-            else:
-                rms = small.tile([P, 2], F32, name="rms")
-                nc.scalar.activation(out=rms[:], in_=ss[:], func=ACT.Sqrt, scale=1.0 / KVR, bias=eps_t[:])
-                nc.vector.reciprocal(out=rstd[:], in_=rms[:])
-            st["rstd", n] = rstd
+            nc.scalar.activation(out=rstd[:], in_=sums[:], func=ACT.Abs_reciprocal_sqrt, scale=1.0 / KVR, bias=eps_t[:])
+            live["rstd", n] = rstd
 
         def normalise(n, a):
             if a == 0:
-                st["cn", n] = work.tile([P, 2, KVR], BF16, name="cn")
-            nc.vector.scalar_tensor_tensor(out=st["cn", n][:, a, :], in0=st["cb", n, a][:], scalar=st["rstd", n][:, a:a + 1],
-                                           in1=gain_b[:], op0=ALU.mult, op1=ALU.mult)
+                live["cn", n] = work.tile([P, 2, KVR], BF16, name="cn")
+            nc.vector.scalar_tensor_tensor(out=live["cn", n][:, a, :], in0=live["c", n, a][:],
+                                           scalar=live["rstd", n][:, a:a + 1], in1=gain[:], op0=ALU.mult, op1=ALU.mult)
 
         def transpose_cn(n):
-            cn = st["cn", n]
-            ct = psum.tile([P, 2, 4, P], BF16, name="ct")
+            cn = live["cn", n]
+            cnt = psum.tile([P, 2, PACK, P], BF16, name="cnt")
             for a in range(2):
-                for t in range(4):
-                    nc.tensor.transpose(ct[:, a, t, :], cn[:, a, P * t:P * t + P], ident_b[:])
-            st["ct", n] = ct
+                for t in range(PACK):
+                    nc.tensor.transpose(cnt[:, a, t, :], cn[:, a, P * t:P * t + P], ident_b[:])
+            live["cnt", n] = cnt
 
-        def exit_cn(n):
-            dst = grouped(n + 3)[:, PW * 4:2 * PW * 4].rearrange("p (a r t) -> p a r t", a=2, t=4)
-            src = st["ct", n][:].rearrange("p a t r -> p a r t")
-            nc.scalar.copy(out=dst, in_=src)
+        def copy_cn(n):
+            dst = grouped(n + 3)[:, PW * PACK:2 * PW * PACK].rearrange("p (a r t) -> p a r t", a=2, t=PACK)
+            src = live["cnt", n][:].rearrange("p a t r -> p a r t")
+            if n >= NPAIR - 2:
+                nc.scalar.copy(out=dst, in_=src)
+            else:
+                nc.vector.tensor_copy(out=dst, in_=src)
 
         def matmul_2(n):
-            cod, scl = st["cod", n + 3]
-            pv = psum.tile([P, 2, H * VD], F32, name="pv")
-            pk = psum.tile([P, 2, H * NOPE], F32, name="pk")
+            words, scales = live["quantised", n + 3]
+            v_ps = psum.tile([P, 2, H * VD], F32, name="v_ps")
+            k_ps = psum.tile([P, 2, H * NOPE], F32, name="k_ps")
             for a in range(2):
                 lo = PW + P * a
-                nc.tensor.matmul_mx(out=pv[:, a, :], lhsT=cod[:, lo:lo + P].bitcast(FP8X4), lhsT_scale=scl[:, lo:lo + P],
-                                    rhs=wbvq[:].bitcast(FP8X4), rhs_scale=wbvs[:], start=True, stop=True)
-                nc.tensor.matmul_mx(out=pk[:, a, :], lhsT=cod[:, lo:lo + P].bitcast(FP8X4), lhsT_scale=scl[:, lo:lo + P],
-                                    rhs=wbkq[:].bitcast(FP8X4), rhs_scale=wbks[:], start=True, stop=True)
-            st["pv", n] = pv
-            st["pk", n] = pk
+                nc.tensor.matmul_mx(out=v_ps[:, a, :], lhsT=words[:, lo:lo + P].bitcast(FP8X4),
+                                    lhsT_scale=scales[:, lo:lo + P],
+                                    rhs=wv_words[:].bitcast(FP8X4), rhs_scale=wv_scales[:], start=True, stop=True)
+                nc.tensor.matmul_mx(out=k_ps[:, a, :], lhsT=words[:, lo:lo + P].bitcast(FP8X4),
+                                    lhsT_scale=scales[:, lo:lo + P],
+                                    rhs=wk_words[:].bitcast(FP8X4), rhs_scale=wk_scales[:], start=True, stop=True)
+            live["v", n] = v_ps
+            live["k", n] = k_ps
 
-        v_tiles = {}
+        v_chunks = {}
 
-        def store(c, i0, n):
-            lo = c * CH + i0
-            kst = ks_tiles[c]
-            nc.sync.dma_start(out=vv[:, :, lo:lo + n, :], in_=v_tiles[c][:, :, i0:i0 + n, :])
-            nc.sync.dma_start(out=ksv[:, 0, lo:lo + n, :], in_=kst[:, 0, i0:i0 + n, :])
-            nc.sync.dma_start(out=ksv[:, 1, lo:lo + n, 0:NOPE], in_=kst[:, 1, i0:i0 + n, 0:NOPE])
-            nc.sync.dma_start(out=ksv[:, 1, lo:lo + n, NOPE:NOPE + ROPE], in_=kst[:, 0, i0:i0 + n, NOPE:NOPE + ROPE])
+        def store(chunk, i0, count):
+            lo = chunk * CH + i0
+            hi = lo + count
+            ks = ks_chunks[chunk]
+            nc.sync.dma_start(out=v_view[:, :, lo:hi, :], in_=v_chunks[chunk][:, :, i0:i0 + count, :])
+            nc.sync.dma_start(out=ks_view[:, 0, lo:hi, :], in_=ks[:, 0, i0:i0 + count, :])
+            nc.sync.dma_start(out=ks_view[:, 1, lo:hi, 0:NOPE], in_=ks[:, 1, i0:i0 + count, 0:NOPE])
+            nc.sync.dma_start(out=ks_view[:, 1, lo:hi, NOPE:NOPE + ROPE], in_=ks[:, 0, i0:i0 + count, NOPE:NOPE + ROPE])
 
-        def exit_kv(n):
-            c = n // PPC
+        def copy_kv(n):
+            chunk = n // PPC
             i0 = 2 * (n % PPC)
             if n % PPC == 0:
-                v_tiles[c] = vout.tile([P, H, CH, VD], F32, name="vt")
-            vt = v_tiles[c]
-            nc.vector.tensor_copy(out=vt[:, :, i0:i0 + 2, :], in_=st["pv", n][:].rearrange("p a (h d) -> p h a d", h=H))
-            nc.vector.tensor_copy(out=ks_tiles[c][:, :, i0:i0 + 2, 0:NOPE],
-                                  in_=st["pk", n][:].rearrange("p a (h d) -> p h a d", h=H))
-            if c == NCH - 1:
-                store(c, i0, 2)
+                v_chunks[chunk] = vout.tile([P, H, CH, VD], F32, name="v_sb")
+            nc.scalar.copy(out=v_chunks[chunk][:, :, i0:i0 + 2, :],
+                           in_=live["v", n][:].rearrange("p a (h d) -> p h a d", h=H))
+            nc.scalar.copy(out=ks_chunks[chunk][:, :, i0:i0 + 2, 0:NOPE],
+                           in_=live["k", n][:].rearrange("p a (h d) -> p h a d", h=H))
+            if chunk == NCH - 1:
+                store(chunk, i0, 2)
             elif n % PPC == PPC - 1:
-                store(c, 0, CH)
+                store(chunk, 0, CH)
 
-        table_start()
-        prep_wc()
-
-        for k in range(-1, NPAIR + 5):
-            if on(k - 1):
-                matmul_1(k - 1)
-            if on(k - 5):
-                exit_kv(k - 5)
-            if on(k - 4):
-                matmul_2(k - 4)
-            if on(k - 3):
-                exit_cn(k - 3)
-            if on(k - 1):
-                stats(k - 1)
-            if on(k - 2):
-                normalise(k - 2, 0)
-                normalise(k - 2, 1)
-            if on(k + 1):
-                transpose_x(k + 1)
-                if (k + 1) % PPC == PPC - 1 and (k + 1) // PPC + 4 < NCH:
-                    load_x((k + 1) // PPC + 4, [CH])
-            if on(k - 2):
-                transpose_cn(k - 2)
-            if on(k + 1):
-                exit_x(k + 1)
-            if on(k) or on(k - 3):
-                quantise(k)
-            if k == -1:
-                table_end()
-                regroup_wb()
-            if k == 3:
-                quantise_wb()
-            if 0 <= k < NRG:
-                rope(k)
+        reduce_angles()
+        quantise_wkv_c()
+        for m in range(-1, NPAIR + 4):
+            if on(m - 1):
+                matmul_1(m - 1)
+            if on(m - 4):
+                matmul_2(m - 4)
+            if on(m - 1):
+                statistics(m - 1)
+            if on(m - 4):
+                copy_kv(m - 4)
+            if on(m - 2):
+                normalise(m - 2, 0)
+            if on(m - 3):
+                copy_cn(m - 3)
+            if on(m - 2):
+                normalise(m - 2, 1)
+            if on(m + 1):
+                transpose_x(m + 1)
+                if (m + 1) % PPC == PPC - 1 and (m + 1) // PPC + X_BUFS < NCH:
+                    load_x((m + 1) // PPC + X_BUFS, [CH])
+            if on(m - 2):
+                transpose_cn(m - 2)
+            if on(m + 1):
+                copy_x(m + 1)
+            if on(m) or on(m - 3):
+                quantise(m)
+            if m == -1:
+                make_tables()
+            if m == 1:
+                quantise_wkv_b()
+            if 0 <= m < TPP // RG:
+                rotate_keys(m)

from contextlib import ExitStack

import concourse.mybir as mybir
from concourse.masks import make_identity

F32 = mybir.dt.float32
BF16 = mybir.dt.bfloat16
U32 = mybir.dt.uint32
U8 = mybir.dt.uint8
I32 = mybir.dt.int32
FP8X4 = mybir.dt.float8_e4m3fn_x4
ALU = mybir.AluOpType
ACT = mybir.ActivationFunctionType

P = 128
PACK = 4
T = 8192
D = 512
KVR = 512
H = 2
NOPE = 64
VD = 128
ROPE = 64
HALF = ROPE // 2
EPS = 1.1920928955078125e-07
PI = 3.141592653589793
TPP = T // P
CH = 8
NCH = TPP // CH
NPAIR = TPP // 2
PPC = CH // 2
PW = 2 * P
RG = 4
X_BUFS = 4

FLOPS = 2 * T * D * KVR + 2 * T * KVR * H * (NOPE + VD)


def tile_deepseekmultiheadattention_pb_t_kernel(tc, x, wkv_c, kv_a_norm_w, wkv_b, k_pe, out_0, out_1):
    nc = tc.nc
    x_view = x.flatten_outer_dims().rearrange("(p i) k -> p i k", i=TPP)
    kpe_view = k_pe.flatten_outer_dims().rearrange("(p i) d -> p i d", i=TPP)
    ks_view = out_0.rearrange("o h (p i) d -> p (o h) i d", i=TPP)
    v_view = out_1.rearrange("o h (p i) d -> p (o h) i d", i=TPP)

    with ExitStack() as ctx:
        const = ctx.enter_context(tc.tile_pool(name="const", bufs=1))
        xin = ctx.enter_context(tc.tile_pool(name="xin", bufs=X_BUFS))
        work = ctx.enter_context(tc.tile_pool(name="work", bufs=3))
        small = ctx.enter_context(tc.tile_pool(name="small", bufs=4))
        vout = ctx.enter_context(tc.tile_pool(name="vout", bufs=3))
        turn = ctx.enter_context(tc.tile_pool(name="turn", bufs=2))
        psum = ctx.enter_context(tc.psum_pool(name="psum", bufs=1))
        ctx.enter_context(tc.manual_schedule())

        x_chunks = {}

        def load_x(chunk, pieces):
            xc = xin.tile([P, CH, D], BF16, name="xc")
            lo = 0
            for count in pieces:
                nc.sync.dma_start(out=xc[:, lo:lo + count, :],
                                  in_=x_view[:, chunk * CH + lo:chunk * CH + lo + count, :])
                lo += count
            x_chunks[chunk] = xc

        wc_raw = const.tile([P, PACK, KVR], BF16, name="wc_raw")
        wb_raw = const.tile([P, PACK, H * (NOPE + VD)], BF16, name="wb_raw")
        gain = const.tile([P, KVR], BF16, name="gain")
        kpe = const.tile([P, TPP, ROPE], BF16, name="kpe")

        load_x(0, [2, CH - 2])
        for u in range(2):
            nc.scalar.dma_start(out=wc_raw[:, 2 * u:2 * u + 2, :],
                                in_=wkv_c[256 * u:256 * u + 256, :].rearrange("(p e) f -> p e f", e=2))
        nc.scalar.dma_start(out=gain[:], in_=kv_a_norm_w.partition_broadcast(P))
        nc.sync.dma_start(out=wb_raw[:], in_=wkv_b.rearrange("(t p) w -> p t w", p=P))
        load_x(1, [CH])
        nc.sync.dma_start(out=kpe[:], in_=kpe_view)
        for chunk in range(2, X_BUFS):
            load_x(chunk, [CH])

        NPOS = NCH + CH
        pos = const.tile([P, NPOS], F32, name="pos")
        nc.gpsimd.iota(pos[:, 0:NCH], pattern=[[CH, NCH]], base=0, channel_multiplier=TPP,
                       allow_small_or_imprecise_dtypes=True)
        nc.gpsimd.iota(pos[:, NCH:NPOS], pattern=[[1, CH]], base=0, channel_multiplier=0,
                       allow_small_or_imprecise_dtypes=True)
        ident_f = const.tile([P, P], F32, name="ident_f")
        make_identity(nc, ident_f[:])
        ident_b = const.tile([P, P], BF16, name="ident_b")
        make_identity(nc, ident_b[:])
        eps_t = const.tile([P, 1], F32, name="eps_t")
        nc.vector.memset(eps_t[:], EPS)
        one_t = const.tile([P, 1], F32, name="one_t")
        nc.vector.memset(one_t[:], 1.0)

        freq = const.tile([P, HALF], F32, name="freq")
        turns = const.tile([P, NPOS, HALF], F32, name="turns")
        whole = const.tile([P, NPOS, HALF], I32, name="whole")
        sin_t = const.tile([P, NPOS, HALF], F32, name="sin_t")
        cos_t = const.tile([P, NPOS, HALF], F32, name="cos_t")
        unused = const.tile([P, 1], F32, name="unused")

        def reduce_angles():
            for j in range(HALF):
                turns_a_position = 10000.0 ** (-j / float(HALF)) / (2.0 * PI)
                if j < HALF // 2:
                    nc.vector.tensor_scalar(out=freq[:, j:j + 1], in0=one_t[:], scalar1=turns_a_position, scalar2=None,
                                            op0=ALU.mult)
                else:
                    nc.scalar.mul(out=freq[:, j:j + 1], in_=one_t[:], mul=turns_a_position)
            nc.vector.tensor_tensor(out=turns[:], in0=pos[:].unsqueeze(2).to_broadcast([P, NPOS, HALF]),
                                    in1=freq[:].unsqueeze(1).to_broadcast([P, NPOS, HALF]), op=ALU.mult)
            nc.vector.tensor_copy(out=whole[:], in_=turns[:])
            nc.vector.tensor_tensor(out=turns[:], in0=turns[:], in1=whole[:], op=ALU.subtract)

        def make_tables():
            nc.scalar.activation(out=sin_t[:], in_=turns[:], func=ACT.Sin, scale=2.0 * PI)
            nc.scalar.activation(out=cos_t[:], in_=turns[:], func=ACT.Sin, scale=PI)
            nc.scalar.activation(out=unused[:], in_=one_t[:], func=ACT.Abs_reciprocal_sqrt)
            nc.gpsimd.tensor_tensor(out=cos_t[:], in0=cos_t[:], in1=cos_t[:], op=ALU.mult)
            nc.gpsimd.tensor_scalar(out=cos_t[:], in0=cos_t[:], scalar1=-2.0, scalar2=1.0, op0=ALU.mult, op1=ALU.add)

        wc_words = const.tile([P, KVR], U32, name="wc_words", align_bytes=64)
        wc_scales = const.tile([P, KVR], U8, name="wc_scales", align_bytes=64)
        wv_words = const.tile([P, H * VD], U32, name="wv_words", align_bytes=64)
        wv_scales = const.tile([P, H * VD], U8, name="wv_scales", align_bytes=64)
        wk_words = const.tile([P, H * NOPE], U32, name="wk_words", align_bytes=64)
        wk_scales = const.tile([P, H * NOPE], U8, name="wk_scales", align_bytes=64)

        def quantise_wkv_c():
            wc_grouped = const.tile([P, KVR, PACK], BF16, name="wc_grouped", align_bytes=64)
            nc.vector.tensor_copy(out=wc_grouped[:], in_=wc_raw[:].rearrange("p t f -> p f t"))
            nc.vector.quantize_mx(out=wc_words[:].bitcast(FP8X4), scales=wc_scales[:],
                                  in_=wc_grouped[:].rearrange("p f t -> p (f t)"))

        def quantise_wkv_b():
            by_head = wb_raw[:].rearrange("p t (h d) -> p t h d", h=H)
            wv_grouped = const.tile([P, H, VD, PACK], BF16, name="wv_grouped", align_bytes=64)
            wk_grouped = const.tile([P, H, NOPE, PACK], BF16, name="wk_grouped", align_bytes=64)
            nc.vector.tensor_copy(out=wv_grouped[:], in_=by_head[:, :, :, NOPE:NOPE + VD].rearrange("p t h d -> p h d t"))
            nc.vector.tensor_copy(out=wk_grouped[:], in_=by_head[:, :, :, 0:NOPE].rearrange("p t h d -> p h d t"))
            nc.vector.quantize_mx(out=wv_words[:].bitcast(FP8X4), scales=wv_scales[:],
                                  in_=wv_grouped[:].rearrange("p h d t -> p (h d t)"))
            nc.vector.quantize_mx(out=wk_words[:].bitcast(FP8X4), scales=wk_scales[:],
                                  in_=wk_grouped[:].rearrange("p h d t -> p (h d t)"))

        ks_chunks = {}
        for chunk in range(NCH):
            ks_chunks[chunk] = const.tile([P, H, CH, NOPE + ROPE], F32, name="ks%d" % chunk)

        def rotate(out_lo, out_hi, src, cos_a, sin_a):
            by_cos = turn.tile([P, RG, 2, HALF], F32, name="by_cos")
            by_sin = turn.tile([P, RG, 2, HALF], F32, name="by_sin")
            nc.gpsimd.tensor_tensor(out=by_cos[:], in0=src, in1=cos_a, op=ALU.mult)
            nc.gpsimd.tensor_tensor(out=by_sin[:], in0=src, in1=sin_a, op=ALU.mult)
            nc.gpsimd.tensor_tensor(out=out_lo, in0=by_cos[:, :, 0, :], in1=by_sin[:, :, 1, :], op=ALU.subtract)
            nc.gpsimd.tensor_tensor(out=out_hi, in0=by_sin[:, :, 0, :], in1=by_cos[:, :, 1, :], op=ALU.add)

        def rotate_keys(g):
            shape = [P, RG, 2, HALF]
            chunk = g * RG // CH
            b = g * RG % CH
            once = turn.tile([P, RG, 2, HALF], F32, name="once")
            rotate(once[:, :, 0, :], once[:, :, 1, :],
                   kpe[:, g * RG:(g + 1) * RG, :].rearrange("p i (s j) -> p i s j", s=2),
                   cos_t[:, NCH + b:NCH + b + RG, :].unsqueeze(2).to_broadcast(shape),
                   sin_t[:, NCH + b:NCH + b + RG, :].unsqueeze(2).to_broadcast(shape))
            rows = ks_chunks[chunk][:, 0, b:b + RG, :]
            rotate(rows[:, :, NOPE:NOPE + HALF], rows[:, :, NOPE + HALF:NOPE + ROPE], once[:],
                   cos_t[:, chunk:chunk + 1, :].unsqueeze(2).to_broadcast(shape),
                   sin_t[:, chunk:chunk + 1, :].unsqueeze(2).to_broadcast(shape))

        live = {}

        def on(n):
            return 0 <= n < NPAIR

        def grouped(period):
            if ("grouped", period) not in live:
                live["grouped", period] = work.tile([P, 2 * PW * PACK], BF16, name="grouped", align_bytes=64)
            return live["grouped", period]

        def transpose_x(n):
            xc = x_chunks[n // PPC]
            xt = psum.tile([P, 2, 2, P], F32, name="xt")
            for a in range(2):
                as_f32 = xc[:, 2 * (n % PPC) + a, :].bitcast(F32)
                for u in range(2):
                    nc.tensor.transpose(xt[:, a, u, :], as_f32[:, P * u:P * u + P], ident_f[:])
            live["xt", n] = xt

        def copy_x(n):
            nc.scalar.copy(out=grouped(n)[:, 0:PW * PACK].bitcast(F32).rearrange("p (a r u) -> p a r u", a=2, u=2),
                           in_=live["xt", n][:].rearrange("p a u r -> p a r u"))

        def quantise(period):
            lo = 0 if on(period) else PW
            hi = 2 * PW if on(period - 3) else PW
            words = work.tile([P, 2 * PW], U32, name="words", align_bytes=64)
            scales = work.tile([P, 2 * PW], U8, name="scales", align_bytes=64)
            nc.vector.quantize_mx(out=words[:, lo:hi].bitcast(FP8X4), scales=scales[:, lo:hi],
                                  in_=grouped(period)[:, PACK * lo:PACK * hi])
            live["quantised", period] = (words, scales)

        def matmul_1(n):
            words, scales = live["quantised", n]
            for a in range(2):
                c_ps = psum.tile([P, KVR], F32, name="c_ps", bufs=4)
                nc.tensor.matmul_mx(out=c_ps[:], lhsT=words[:, P * a:P * a + P].bitcast(FP8X4),
                                    lhsT_scale=scales[:, P * a:P * a + P],
                                    rhs=wc_words[:].bitcast(FP8X4), rhs_scale=wc_scales[:], start=True, stop=True)
                live["c", n, a] = c_ps

        def statistics(n):
            sums = small.tile([P, 2], F32, name="sums")
            for a in range(2):
                squares = work.tile([P, KVR], BF16, name="squares")
                nc.scalar.activation(out=squares[:], in_=live["c", n, a][:], func=ACT.Square, accum_out=sums[:, a:a + 1])
            rstd = small.tile([P, 2], F32, name="rstd")
            nc.scalar.activation(out=rstd[:], in_=sums[:], func=ACT.Abs_reciprocal_sqrt, scale=1.0 / KVR, bias=eps_t[:])
            live["rstd", n] = rstd

        def normalise(n, a):
            if a == 0:
                live["cn", n] = work.tile([P, 2, KVR], BF16, name="cn")
            nc.vector.scalar_tensor_tensor(out=live["cn", n][:, a, :], in0=live["c", n, a][:],
                                           scalar=live["rstd", n][:, a:a + 1], in1=gain[:], op0=ALU.mult, op1=ALU.mult)

        def transpose_cn(n):
            cn = live["cn", n]
            cnt = psum.tile([P, 2, PACK, P], BF16, name="cnt")
            for a in range(2):
                for t in range(PACK):
                    nc.tensor.transpose(cnt[:, a, t, :], cn[:, a, P * t:P * t + P], ident_b[:])
            live["cnt", n] = cnt

        def copy_cn(n):
            dst = grouped(n + 3)[:, PW * PACK:2 * PW * PACK].rearrange("p (a r t) -> p a r t", a=2, t=PACK)
            src = live["cnt", n][:].rearrange("p a t r -> p a r t")
            if n >= NPAIR - 2:
                nc.scalar.copy(out=dst, in_=src)
            else:
                nc.vector.tensor_copy(out=dst, in_=src)

        def matmul_2(n):
            words, scales = live["quantised", n + 3]
            v_ps = psum.tile([P, 2, H * VD], F32, name="v_ps")
            k_ps = psum.tile([P, 2, H * NOPE], F32, name="k_ps")
            for a in range(2):
                lo = PW + P * a
                nc.tensor.matmul_mx(out=v_ps[:, a, :], lhsT=words[:, lo:lo + P].bitcast(FP8X4),
                                    lhsT_scale=scales[:, lo:lo + P],
                                    rhs=wv_words[:].bitcast(FP8X4), rhs_scale=wv_scales[:], start=True, stop=True)
                nc.tensor.matmul_mx(out=k_ps[:, a, :], lhsT=words[:, lo:lo + P].bitcast(FP8X4),
                                    lhsT_scale=scales[:, lo:lo + P],
                                    rhs=wk_words[:].bitcast(FP8X4), rhs_scale=wk_scales[:], start=True, stop=True)
            live["v", n] = v_ps
            live["k", n] = k_ps

        v_chunks = {}

        def store(chunk, i0, count):
            lo = chunk * CH + i0
            hi = lo + count
            ks = ks_chunks[chunk]
            nc.sync.dma_start(out=v_view[:, :, lo:hi, :], in_=v_chunks[chunk][:, :, i0:i0 + count, :])
            nc.sync.dma_start(out=ks_view[:, 0, lo:hi, :], in_=ks[:, 0, i0:i0 + count, :])
            nc.sync.dma_start(out=ks_view[:, 1, lo:hi, 0:NOPE], in_=ks[:, 1, i0:i0 + count, 0:NOPE])
            nc.sync.dma_start(out=ks_view[:, 1, lo:hi, NOPE:NOPE + ROPE], in_=ks[:, 0, i0:i0 + count, NOPE:NOPE + ROPE])

        def copy_kv(n):
            chunk = n // PPC
            i0 = 2 * (n % PPC)
            if n % PPC == 0:
                v_chunks[chunk] = vout.tile([P, H, CH, VD], F32, name="v_sb")
            nc.scalar.copy(out=v_chunks[chunk][:, :, i0:i0 + 2, :],
                           in_=live["v", n][:].rearrange("p a (h d) -> p h a d", h=H))
            nc.scalar.copy(out=ks_chunks[chunk][:, :, i0:i0 + 2, 0:NOPE],
                           in_=live["k", n][:].rearrange("p a (h d) -> p h a d", h=H))
            if chunk == NCH - 1:
                store(chunk, i0, 2)
            elif n % PPC == PPC - 1:
                store(chunk, 0, CH)

        reduce_angles()
        quantise_wkv_c()
        for m in range(-1, NPAIR + 4):
            if on(m - 1):
                matmul_1(m - 1)
            if on(m - 4):
                matmul_2(m - 4)
            if on(m - 1):
                statistics(m - 1)
            if on(m - 4):
                copy_kv(m - 4)
            if on(m - 2):
                normalise(m - 2, 0)
            if on(m - 3):
                copy_cn(m - 3)
            if on(m - 2):
                normalise(m - 2, 1)
            if on(m + 1):
                transpose_x(m + 1)
                if (m + 1) % PPC == PPC - 1 and (m + 1) // PPC + X_BUFS < NCH:
                    load_x((m + 1) // PPC + X_BUFS, [CH])
            if on(m - 2):
                transpose_cn(m - 2)
            if on(m + 1):
                copy_x(m + 1)
            if on(m) or on(m - 3):
                quantise(m)
            if m == -1:
                make_tables()
            if m == 1:
                quantise_wkv_b()
            if 0 <= m < TPP // RG:
                rotate_keys(m)
